import numpy as np
import ml_dtypes


def mxq(x, axis, fmt="e4m3"):
    dtype, down = {"e4m3": (ml_dtypes.float8_e4m3fn, 7), "e5m2": (ml_dtypes.float8_e5m2, 14)}[fmt]
    v = np.moveaxis(np.asarray(x, np.float32).astype(ml_dtypes.bfloat16).astype(np.float64), axis, -1)
    blocks = v.reshape(v.shape[:-1] + (-1, 32))
    amax = np.abs(blocks).max(-1, keepdims=True)
    byte = np.maximum(np.where(amax > 0, np.frexp(amax)[1] - 1 + 127, 0) - down, 1)
    scale = np.exp2(byte - 127.0)
    codes = (blocks / scale).astype(np.float32).astype(dtype).astype(np.float64)
    return np.moveaxis((codes * scale).reshape(v.shape), -1, axis)


WIDE = False


def mx_kscale(k):
    if not WIDE:
        return np.ones(k)
    levels = np.array([10, -10, 5, -5, 0])
    if k % 512:
        return np.exp2(np.random.permutation(np.resize(levels, k // 32))).repeat(32)
    a = np.empty((k // 512, 16))
    for p in range(k // 512):
        a[p, :8] = np.random.permutation(np.resize(levels, 8))
        for g in range(8):
            far = levels[np.abs(levels - a[p, g]) >= 10]
            a[p, g + 8] = far[np.random.randint(len(far))]
    return np.exp2(a.ravel()).repeat(32)


BF16 = ml_dtypes.bfloat16


def bf(x):
    return np.asarray(x, np.float32).astype(BF16)


def f64(x):
    return np.asarray(x).astype(np.float64)


B, N, IN_DIM, OUT_DIM, K = 4, 1024, 1024, 128, 3
EPS = 1e-6
SIG = 2.0


def laplacian(adj):
    d = adj.sum(axis=2)
    r = (d + EPS) ** -0.5
    return np.eye(N)[None] - r[:, :, None] * adj * r[:, None, :]


def setup_inputs():
    s, u = mx_kscale(N), mx_kscale(IN_DIM)
    sn = s / s.max()
    return {"x": bf(np.random.standard_normal((B, N, IN_DIM)) * sn[:, None] * u),
            "tx1": bf(np.random.standard_normal((B, N, IN_DIM)) * sn[:, None] * u),
            "adj": bf(np.exp(SIG * np.random.standard_normal((B, N, N)) - SIG * SIG / 2.0) / N * (s * s)[:, None]),
            "W": bf(np.random.standard_normal((K, IN_DIM, OUT_DIM)) / np.sqrt(IN_DIM) / u[:, None]),
            "b": bf(np.random.standard_normal((K, OUT_DIM)) * 0.3)}


def reference(x, tx1, adj, W, b):
    x, tx1, b = f64(x), f64(tx1), f64(b)
    Wq = mxq(f64(W), 1, "e4m3")
    L = laplacian(f64(adj))
    out = (mxq(x, 2, "e4m3") @ Wq[0]) + b[0] + (mxq(tx1, 2, "e4m3") @ Wq[1]) + b[1]
    tx2 = 2.0 * (mxq(L, 2, "e4m3") @ mxq(tx1, 1, "e4m3")) - x
    out = out + (mxq(tx2, 2, "e4m3") @ Wq[2]) + b[2]
    return np.maximum(out, 0.0)

@@ -1,0 +1,421 @@
+from contextlib import ExitStack
+
+import concourse.mybir as mybir
+from concourse.masks import make_identity
+
+F32 = mybir.dt.float32
+BF16 = mybir.dt.bfloat16
+U32 = mybir.dt.uint32
+U8 = mybir.dt.uint8
+FP8X4 = mybir.dt.float8_e4m3fn_x4
+ALU = mybir.AluOpType
+ACT = mybir.ActivationFunctionType
+
+P = 128
+GRAPHS = 4
+NODES = 1024
+FEATS = 1024
+OUT = 128
+ORDERS = 3
+EPS = 1e-6
+
+BLOCK_BF16 = 16
+PACK = 4
+K_PASS = P * PACK
+PASSES = NODES // K_PASS
+CHUNKS = NODES // P
+HALF = CHUNKS // PASSES
+ALL_CHUNKS = GRAPHS * CHUNKS
+
+AT_STORE = -1
+AT_RELU = 0
+AT_OUTPUT = 1
+AT_TERM = 2
+AT_SECOND_ORDER = 3
+AT_QUANTISE = 4
+AT_TRANSPOSE = 5
+AT_LAP = 8
+AT_SPREAD = AT_LAP + 1
+AT_RECIPROCAL = AT_LAP + 2
+AT_ROOT = AT_LAP + 3
+AT_ROW_SUMS = AT_ROOT + CHUNKS
+AT_NODE_QUANTISE = AT_SECOND_ORDER + 1 + CHUNKS
+AT_NODE_REGROUP = AT_NODE_QUANTISE + 1
+X, TX1, LAP, TX2 = 0, 1, 2, 3
+TX2_LAG = AT_QUANTISE - AT_TERM
+EARLY = 4
+LOAD_AHEAD = 4
+ADJ_BUFS = 6
+TX1_BUFS = 4
+X_BUFS = 2
+assert AT_ROW_SUMS + LOAD_AHEAD <= AT_TRANSPOSE + (ADJ_BUFS - 1) * HALF
+assert AT_NODE_REGROUP + LOAD_AHEAD <= AT_TRANSPOSE + (TX1_BUFS - 1) * HALF
+assert AT_TRANSPOSE + LOAD_AHEAD <= AT_TRANSPOSE + (X_BUFS - 1) * HALF
+
+FLOPS = GRAPHS * (2 * NODES * NODES * FEATS + ORDERS * 2 * NODES * FEATS * OUT)
+
+
+def tile_cheblayer_pb_t_kernel(tc, x, tx1, adj, W, b, out):
+    nc = tc.nc
+    with ExitStack() as stack:
+        pool = lambda name, bufs: stack.enter_context(tc.tile_pool(name=name, bufs=bufs))
+        const = pool("const", 1)
+        adj_pool = pool("adj", ADJ_BUFS)
+        tx1_pool = pool("tx1", TX1_BUFS)
+        x_pool = pool("x", X_BUFS)
+        graph_pool = pool("graph", 3)
+        node_pool = pool("node", 5)
+        short = pool("short", 3)
+        grouped_pool = pool("grouped", 5)
+        codes_pool = pool("codes", 4)
+        psum_t = stack.enter_context(tc.psum_pool(name="psum_t", bufs=4))
+        psum_m = stack.enter_context(tc.psum_pool(name="psum_m", bufs=2))
+        psum_o = stack.enter_context(tc.psum_pool(name="psum_o", bufs=2))
+        stack.enter_context(tc.manual_schedule())
+
+        ident = const.tile([P, P], F32)
+        make_identity(nc, ident[:])
+        ident_bf = const.tile([P, P], BF16)
+        make_identity(nc, ident_bf[:])
+        eps = const.tile([P, 1], F32)
+        nc.vector.memset(eps[:], EPS)
+        warm = const.tile([P, 1], F32)
+        nc.scalar.activation(out=warm[:], in_=eps[:], func=ACT.Sqrt)
+
+        halves = {}
+
+        def load_half(name, src, tile_pool, q):
+            g, h = q // CHUNKS, (q % CHUNKS) // HALF
+            t = tile_pool.tile([P, HALF, FEATS], BF16, name=name)
+            rows = src[g, h * K_PASS : (h + 1) * K_PASS, :].rearrange("(p t) f -> p t f", t=PACK)
+            for c in range(0, HALF, 2):
+                nc.sync.dma_start(out=t[:, c : c + 2, :], in_=rows[:, c : c + 2, :])
+            halves[(name, g, h)] = t
+
+        def half_of(name, s):
+            return halves[(name, s // CHUNKS, (s % CHUNKS) // HALF)]
+
+        w_raw = const.tile([P, ORDERS * PASSES, PACK, OUT], BF16)
+        w_grouped = const.tile([P, ORDERS * PASSES, OUT, PACK], BF16, align_bytes=64)
+        w_codes = const.tile([P, ORDERS, PASSES, OUT], U32, align_bytes=64)
+        w_scales = const.tile([P, ORDERS, PASSES, OUT], U8, align_bytes=64)
+        b_rows = const.tile([P, P], BF16)
+        b_terms = const.tile([P, ORDERS], F32)
+        bias = const.tile([P, 1], F32)
+
+        def load_weights():
+            nc.sync.dma_start(
+                out=w_raw[:].rearrange("p a t o -> p a (t o)"),
+                in_=W.rearrange("k (a p t) o -> p (k a) (t o)", p=P, t=PACK),
+            )
+            nc.vector.memset(b_rows[:], 0.0)
+            nc.sync.dma_start(out=b_rows[0:ORDERS, :], in_=b)
+
+        def quantise_weights():
+            nc.vector.tensor_copy(out=w_grouped[:], in_=w_raw[:].rearrange("p a t o -> p a o t"))
+            for k in range(ORDERS):
+                nc.vector.quantize_mx(
+                    out=w_codes[:, k].rearrange("p a o -> p (a o)").bitcast(FP8X4),
+                    scales=w_scales[:, k].rearrange("p a o -> p (a o)"),
+                    in_=w_grouped[:, k * PASSES : (k + 1) * PASSES].rearrange("p a o t -> p (a o t)"),
+                )
+            b_cols = psum_t.tile([P, P], BF16, name="bank")
+            nc.tensor.transpose(out=b_cols[:], in_=b_rows[:], identity=ident_bf[:])
+            nc.scalar.activation(out=b_terms[:], in_=b_cols[:, 0:ORDERS], func=ACT.Copy, accum_out=bias[:, 0:1])
+
+        vectors = {g: {} for g in range(GRAPHS)}
+        node_codes = {}
+        node_grouped = {}
+
+        def node_regroup(q):
+            if q % 2 == 0:
+                node_grouped[q // 2] = short.tile([P, 2, 2, P, PACK], BF16, name="node_grouped", align_bytes=64)
+            j = q % HALF
+            features = half_of("tx1", q)[:, :, (j // 2) * K_PASS : (j // 2 + 1) * K_PASS]
+            rows = features.rearrange("p t (m v) -> p v m t", v=PACK)[:, 2 * (j % 2) : 2 * (j % 2) + 2]
+            if q < HALF:
+                nc.vector.tensor_copy(out=node_grouped[q // 2][:, q % 2], in_=rows)
+            else:
+                nc.scalar.copy(out=node_grouped[q // 2][:, q % 2], in_=rows)
+
+        def node_quantise(q):
+            key = (q // CHUNKS, (q % CHUNKS) // HALF)
+            if q % HALF == 1:
+                node_codes[key] = (
+                    node_pool.tile([P, FEATS], U32, name="node_c", align_bytes=64),
+                    node_pool.tile([P, FEATS], U8, name="node_s", align_bytes=64),
+                )
+            codes, scales = node_codes[key]
+            windows = slice((q % HALF - 1) * 2 * P, (q % HALF + 1) * 2 * P)
+            nc.vector.quantize_mx(
+                out=codes[:, windows].bitcast(FP8X4),
+                scales=scales[:, windows],
+                in_=node_grouped[q // 2][:].rearrange("p w e m t -> p (w e m t)"),
+            )
+
+        def row_sums(q):
+            g, k = q // CHUNKS, q % CHUNKS
+            if k == 0:
+                vectors[g]["d"] = graph_pool.tile([P, CHUNKS], F32, name="d")
+            folded = psum_t.tile([P, P], F32, name="bank")
+            for blk in range(CHUNKS):
+                nc.tensor.matmul(
+                    out=folded[:],
+                    lhsT=ident_bf[:],
+                    rhs=half_of("adj", q)[:, q % HALF, blk * P : (blk + 1) * P],
+                    start=(blk == 0),
+                    stop=(blk == CHUNKS - 1),
+                )
+            junk = short.tile([P, P], F32, name="junk")
+            nc.scalar.activation(out=junk[:], in_=folded[:], func=ACT.Copy, accum_out=vectors[g]["d"][:, k : k + 1])
+
+        def vectors_root(g):
+            vectors[g]["root"] = graph_pool.tile([P, CHUNKS], F32, name="root")
+            nc.scalar.activation(out=vectors[g]["root"][:], in_=vectors[g]["d"][:], func=ACT.Sqrt, bias=eps[:, 0:1])
+
+        def vectors_reciprocal(g):
+            v = vectors[g]
+            v["r"] = graph_pool.tile([P, CHUNKS], F32, name="r")
+            nc.vector.reciprocal(out=v["r"][:], in_=v["root"][:])
+            v["neg_r"] = graph_pool.tile([P, CHUNKS], F32, name="neg_r")
+            nc.vector.tensor_scalar_mul(out=v["neg_r"][:], in0=v["r"][:], scalar1=-1.0)
+
+        def load_diagonal(g):
+            vectors[g]["a_diag"] = graph_pool.tile([P, 2, BLOCK_BF16], BF16, name="a_diag")
+            diagonal = adj[g].rearrange("i j -> (i j)")[0 : NODES * NODES : NODES + 1]
+            with nc.allow_non_contiguous_dma(reason="1,024 single elements, one from each row of adj"):
+                for h in range(PASSES):
+                    nc.sync.dma_start(
+                        out=vectors[g]["a_diag"][:, h, 0:HALF],
+                        in_=diagonal.rearrange("(h p t) -> h p t", p=P, t=HALF)[h],
+                    )
+
+        def vectors_diagonal(g):
+            v = vectors[g]
+            small = lambda name, dtype: graph_pool.tile([P, CHUNKS], dtype, name=name)
+            half_product, product, stored, one_more = (
+                small("half_product", F32), small("product", F32), small("stored", BF16), small("one_more", F32)
+            )
+            v["eye_fix"] = small("eye_fix", F32)
+            by_half = lambda ap: ap.rearrange("p (h t) -> p h t", t=HALF)
+            nc.gpsimd.tensor_tensor(
+                out=by_half(half_product[:]),
+                in0=v["a_diag"][:, :, 0:HALF],
+                in1=by_half(v["neg_r"][:]),
+                op=ALU.mult,
+            )
+            nc.gpsimd.tensor_tensor(out=product[:], in0=half_product[:], in1=v["r"][:], op=ALU.mult)
+            nc.gpsimd.tensor_copy(out=stored[:], in_=product[:])
+            nc.gpsimd.tensor_scalar_add(out=one_more[:], in0=product[:], scalar1=1.0)
+            nc.gpsimd.tensor_tensor(out=v["eye_fix"][:], in0=one_more[:], in1=stored[:], op=ALU.subtract)
+
+        def vectors_spread(g):
+            v = vectors[g]
+            v["r_cols"] = graph_pool.tile([P, NODES], F32, name="r_cols")
+            for h in range(PASSES):
+                spread = psum_t.tile([P, HALF, P], F32, name="bank")
+                for j in range(HALF):
+                    k = h * HALF + j
+                    nc.tensor.transpose(
+                        out=spread[:, j, :], in_=v["r"][:, k : k + 1].to_broadcast([P, P]), identity=ident[:]
+                    )
+                nc.scalar.copy(
+                    out=v["r_cols"][:, h * K_PASS : (h + 1) * K_PASS].rearrange("p (n t) -> p n t", t=HALF),
+                    in_=spread[:].rearrange("p t n -> p n t"),
+                )
+
+        chunks = {s: {} for s in range(ALL_CHUNKS + TX2_LAG)}
+
+        def grouped_of(s):
+            if "grouped" not in chunks[s]:
+                chunks[s]["grouped"] = grouped_pool.tile([P, 4, PASSES, P, PACK], BF16, name="grouped", align_bytes=64)
+            return chunks[s]["grouped"]
+
+        def transposed_words(src_half, j):
+            words = src_half[:].bitcast(F32)
+            bank = psum_t.tile([P, PACK, P], F32, name="bank")
+            for a in range(PASSES):
+                for u in range(2):
+                    every_second = words[:, j, 2 * P * a + u : 2 * P * (a + 1) : 2]
+                    nc.tensor.transpose(out=bank[:, 2 * a + u, :], in_=every_second, identity=ident[:])
+            return bank
+
+        def feat_transpose(s):
+            words = grouped_of(s)[:].bitcast(F32)
+            for section, name in ((X, "x"), (TX1, "tx1")):
+                bank = transposed_words(half_of(name, s), s % HALF)
+                nc.scalar.copy(out=words[:, section], in_=bank[:].rearrange("p (a u) i -> p a i u", u=2))
+
+        def quantise(s, first, last):
+            t = chunks[s]
+            if "codes" not in t:
+                t["codes"] = codes_pool.tile([P, 4, PASSES, P], U32, name="codes", align_bytes=64)
+                t["scales"] = codes_pool.tile([P, 4, PASSES, P], U8, name="scales", align_bytes=64)
+            nc.vector.quantize_mx(
+                out=t["codes"][:, first:last].rearrange("p m a i -> p (m a i)").bitcast(FP8X4),
+                scales=t["scales"][:, first:last].rearrange("p m a i -> p (m a i)"),
+                in_=t["grouped"][:, first:last].rearrange("p m a i t -> p (m a i t)"),
+            )
+
+        def lap_rows(s):
+            k = s % CHUNKS
+            v = vectors[s // CHUNKS]
+            row = half_of("adj", s)[:, s % HALF, :]
+            nc.vector.scalar_tensor_tensor(
+                out=row, in0=row, scalar=v["neg_r"][:, k : k + 1], in1=v["r_cols"][:], op0=ALU.mult, op1=ALU.mult
+            )
+
+        def lap_add_eye(s):
+            k = s % CHUNKS
+            row = half_of("adj", s)[:, s % HALF, :]
+            diag_cols = row.rearrange("p (h n t) -> p h n t", n=P, t=HALF)[:, k // HALF, :, k % HALF]
+            nc.vector.scalar_tensor_tensor(
+                out=diag_cols,
+                in0=ident[:],
+                scalar=vectors[s // CHUNKS]["eye_fix"][:, k : k + 1],
+                in1=diag_cols,
+                op0=ALU.mult,
+                op1=ALU.add,
+            )
+
+        def lap_transpose(s):
+            bank = transposed_words(half_of("adj", s), s % HALF)
+            pairs = bank[:].bitcast(BF16).rearrange("p (a u) (i e) -> p a i u e", u=2, e=2)
+            for a in range(PASSES):
+                nc.scalar.copy(out=grouped_of(s)[:, LAP, a].rearrange("p i (u e) -> p i u e", e=2), in_=pairs[:, a])
+
+        def second_order_products(s):
+            t = chunks[s]
+            t["acc"] = []
+            for a in range(PASSES):
+                acc = psum_m.tile([P, PACK, P], F32, name="acc")
+                t["acc"].append(acc)
+                for v in range(PACK):
+                    cols = slice((a * PACK + v) * P, (a * PACK + v + 1) * P)
+                    for h in range(PASSES):
+                        codes, scales = node_codes[(s // CHUNKS, h)]
+                        nc.tensor.matmul_mx(
+                            out=acc[:, v, :],
+                            lhsT=codes[:, cols].bitcast(FP8X4),
+                            lhsT_scale=scales[:, cols],
+                            rhs=t["codes"][:, LAP, h, :].bitcast(FP8X4),
+                            rhs_scale=t["scales"][:, LAP, h, :],
+                            start=(h == 0),
+                            stop=(h == PASSES - 1),
+                        )
+
+        def second_order_term(s, a):
+            nc.vector.scalar_tensor_tensor(
+                out=grouped_of(s + TX2_LAG)[:, TX2, a],
+                in0=chunks[s]["acc"][a][:].rearrange("p v i -> p i v"),
+                scalar=2.0,
+                in1=grouped_of(s)[:, X, a],
+                op0=ALU.mult,
+                op1=ALU.subtract,
+            )
+
+        pair_acc = {}
+
+        def output_products(s):
+            t = chunks[s]
+            if s % 2 == 0:
+                pair_acc[s // 2] = psum_o.tile([P, 2, P], F32, name="out_acc")
+            later = chunks[s + TX2_LAG]
+            operands = [
+                (t["codes"][:, X], t["scales"][:, X]),
+                (t["codes"][:, TX1], t["scales"][:, TX1]),
+                (later["codes"][:, TX2], later["scales"][:, TX2]),
+            ]
+            for k, (codes, scales) in enumerate(operands):
+                for a in range(PASSES):
+                    nc.tensor.matmul_mx(
+                        out=pair_acc[s // 2][:, s % 2, :],
+                        lhsT=w_codes[:, k, a, :].bitcast(FP8X4),
+                        lhsT_scale=w_scales[:, k, a, :],
+                        rhs=codes[:, a, :].bitcast(FP8X4),
+                        rhs_scale=scales[:, a, :],
+                        start=(k == 0 and a == 0),
+                        stop=(k == ORDERS - 1 and a == PASSES - 1),
+                    )
+
+        def output_relu(s):
+            chunks[s]["relu"] = short.tile([P, 2, P], F32, name="relu")
+            nc.scalar.activation(out=chunks[s]["relu"][:], in_=pair_acc[s // 2][:], func=ACT.Relu, bias=bias[:, 0:1])
+
+        def output_store(s):
+            g, h, t = s // CHUNKS, (s % CHUNKS) // HALF, s % HALF - 1
+            bank = psum_t.tile([P, 2, OUT], F32, name="bank")
+            for e in range(2):
+                nc.tensor.transpose(out=bank[:, e, :], in_=chunks[s]["relu"][:, e, :], identity=ident[:])
+            result = short.tile([P, 2, OUT], F32, name="result")
+            nc.scalar.copy(out=result[:], in_=bank[:])
+            rows = out[g, h * K_PASS : (h + 1) * K_PASS, :].rearrange("(p t) o -> p t o", t=HALF)
+            nc.sync.dma_start(out=rows[:, t : t + 2, :], in_=result[:])
+
+        valid = lambda s: 0 <= s < ALL_CHUNKS
+        first_of_half = lambda s: valid(s) and s % HALF == 0
+        first_of_graph = lambda s: valid(s) and s % CHUNKS == 0
+        second_of_pair = lambda s: valid(s) and s % 2 == 1
+
+        def lap_side(m):
+            if m + EARLY < CHUNKS:
+                return m + EARLY
+            return m if m >= CHUNKS else -1
+
+        first_step = -(AT_ROW_SUMS + LOAD_AHEAD + EARLY)
+        for n in range(first_step, ALL_CHUNKS - AT_STORE):
+            if first_of_half(n + AT_TRANSPOSE + LOAD_AHEAD):
+                load_half("x", x, x_pool, n + AT_TRANSPOSE + LOAD_AHEAD)
+            if n + AT_TRANSPOSE + LOAD_AHEAD == 0:
+                load_weights()
+            if first_of_half(n + AT_NODE_REGROUP + LOAD_AHEAD):
+                load_half("tx1", tx1, tx1_pool, n + AT_NODE_REGROUP + LOAD_AHEAD)
+            if first_of_half(lap_side(n + AT_ROW_SUMS + LOAD_AHEAD)):
+                load_half("adj", adj, adj_pool, lap_side(n + AT_ROW_SUMS + LOAD_AHEAD))
+            if first_of_graph(lap_side(n + AT_ROW_SUMS)):
+                load_diagonal(lap_side(n + AT_ROW_SUMS) // CHUNKS)
+
+            if first_of_graph(lap_side(n + AT_ROOT)):
+                vectors_root(lap_side(n + AT_ROOT) // CHUNKS)
+            if first_of_graph(lap_side(n + AT_SPREAD)):
+                vectors_spread(lap_side(n + AT_SPREAD) // CHUNKS)
+                vectors_diagonal(lap_side(n + AT_SPREAD) // CHUNKS)
+
+            if second_of_pair(n + AT_RELU):
+                output_relu(n + AT_RELU)
+            if valid(n + AT_NODE_REGROUP):
+                node_regroup(n + AT_NODE_REGROUP)
+
+            if valid(n + AT_OUTPUT):
+                output_products(n + AT_OUTPUT)
+            if valid(lap_side(n + AT_ROW_SUMS)):
+                row_sums(lap_side(n + AT_ROW_SUMS))
+            if second_of_pair(n + AT_STORE):
+                output_store(n + AT_STORE)
+            if valid(n + AT_TRANSPOSE):
+                feat_transpose(n + AT_TRANSPOSE)
+                lap_transpose(n + AT_TRANSPOSE)
+
+            if n + AT_QUANTISE == 0:
+                quantise_weights()
+            if first_of_graph(lap_side(n + AT_RECIPROCAL)):
+                vectors_reciprocal(lap_side(n + AT_RECIPROCAL) // CHUNKS)
+            if valid(lap_side(n + AT_LAP)):
+                lap_rows(lap_side(n + AT_LAP))
+            if valid(n + AT_TERM):
+                second_order_term(n + AT_TERM, 0)
+                second_order_term(n + AT_TERM, 1)
+            if valid(lap_side(n + AT_LAP)):
+                lap_add_eye(lap_side(n + AT_LAP))
+            if valid(n + AT_QUANTISE) and valid(n + AT_TERM):
+                quantise(n + AT_QUANTISE, X, TX2 + 1)
+            elif valid(n + AT_QUANTISE):
+                quantise(n + AT_QUANTISE, X, TX1 + 1)
+                quantise(n + AT_QUANTISE, LAP, LAP + 1)
+            elif valid(n + AT_TERM):
+                quantise(n + AT_QUANTISE, TX2, TX2 + 1)
+            if second_of_pair(n + AT_NODE_QUANTISE):
+                node_quantise(n + AT_NODE_QUANTISE)
+
+            if valid(n + AT_SECOND_ORDER):
+                second_order_products(n + AT_SECOND_ORDER)

@@ -34,7 +34,7 @@ AT_TERM = 2
 AT_SECOND_ORDER = 3
 AT_QUANTISE = 4
 AT_TRANSPOSE = 5
-AT_LAP = 8
+AT_LAP = 6
 AT_SPREAD = AT_LAP + 1
 AT_RECIPROCAL = AT_LAP + 2
 AT_ROOT = AT_LAP + 3
@@ -43,12 +43,12 @@ AT_NODE_QUANTISE = AT_SECOND_ORDER + 1 + CHUNKS
 AT_NODE_REGROUP = AT_NODE_QUANTISE + 1
 X, TX1, LAP, TX2 = 0, 1, 2, 3
 TX2_LAG = AT_QUANTISE - AT_TERM
-EARLY = 4
 LOAD_AHEAD = 4
-ADJ_BUFS = 6
+ADJ_BUFS = 5
+LAP_BUFS = AT_LAP - AT_TRANSPOSE + 1
 TX1_BUFS = 4
 X_BUFS = 2
-assert AT_ROW_SUMS + LOAD_AHEAD <= AT_TRANSPOSE + (ADJ_BUFS - 1) * HALF
+assert AT_ROW_SUMS + LOAD_AHEAD <= AT_LAP + (ADJ_BUFS - 1) * HALF
 assert AT_NODE_REGROUP + LOAD_AHEAD <= AT_TRANSPOSE + (TX1_BUFS - 1) * HALF
 assert AT_TRANSPOSE + LOAD_AHEAD <= AT_TRANSPOSE + (X_BUFS - 1) * HALF
 
@@ -66,6 +66,7 @@ def tile_cheblayer_pb_t_kernel(tc, x, tx1, adj, W, b, out):
         graph_pool = pool("graph", 3)
         node_pool = pool("node", 5)
         short = pool("short", 3)
+        lap_pool = pool("lap", LAP_BUFS)
         grouped_pool = pool("grouped", 5)
         codes_pool = pool("codes", 4)
         psum_t = stack.enter_context(tc.psum_pool(name="psum_t", bufs=4))
@@ -133,7 +134,7 @@ def tile_cheblayer_pb_t_kernel(tc, x, tx1, adj, W, b, out):
             j = q % HALF
             features = half_of("tx1", q)[:, :, (j // 2) * K_PASS : (j // 2 + 1) * K_PASS]
             rows = features.rearrange("p t (m v) -> p v m t", v=PACK)[:, 2 * (j % 2) : 2 * (j % 2) + 2]
-            if q < HALF:
+            if q < CHUNKS:
                 nc.vector.tensor_copy(out=node_grouped[q // 2][:, q % 2], in_=rows)
             else:
                 nc.scalar.copy(out=node_grouped[q // 2][:, q % 2], in_=rows)
@@ -157,17 +158,28 @@ def tile_cheblayer_pb_t_kernel(tc, x, tx1, adj, W, b, out):
             g, k = q // CHUNKS, q % CHUNKS
             if k == 0:
                 vectors[g]["d"] = graph_pool.tile([P, CHUNKS], F32, name="d")
-            folded = psum_t.tile([P, P], F32, name="bank")
-            for blk in range(CHUNKS):
-                nc.tensor.matmul(
-                    out=folded[:],
-                    lhsT=ident_bf[:],
-                    rhs=half_of("adj", q)[:, q % HALF, blk * P : (blk + 1) * P],
-                    start=(blk == 0),
-                    stop=(blk == CHUNKS - 1),
+            d = vectors[g]["d"][:, k : k + 1]
+            row = half_of("adj", q)[:, q % HALF, :]
+            if g == 0 and k % 2 == 0:
+                junk = short.tile([P, NODES], BF16, name="junk_row")
+                nc.vector.tensor_scalar(
+                    out=junk[:], in0=row, scalar1=1.0, scalar2=None, op0=ALU.mult, op1=ALU.add, accum_out=d
                 )
-            junk = short.tile([P, P], F32, name="junk")
-            nc.scalar.activation(out=junk[:], in_=folded[:], func=ACT.Copy, accum_out=vectors[g]["d"][:, k : k + 1])
+            elif g == 0 or k % 2 == 0:
+                junk = short.tile([P, NODES], BF16, name="junk_row")
+                nc.scalar.activation(out=junk[:], in_=row, func=ACT.Copy, accum_out=d)
+            else:
+                folded = psum_t.tile([P, P], F32, name="bank")
+                for blk in range(CHUNKS):
+                    nc.tensor.matmul(
+                        out=folded[:],
+                        lhsT=ident_bf[:],
+                        rhs=row[:, blk * P : (blk + 1) * P],
+                        start=(blk == 0),
+                        stop=(blk == CHUNKS - 1),
+                    )
+                junk = short.tile([P, P], F32, name="junk")
+                nc.scalar.activation(out=junk[:], in_=folded[:], func=ACT.Copy, accum_out=d)
 
         def vectors_root(g):
             vectors[g]["root"] = graph_pool.tile([P, CHUNKS], F32, name="root")
@@ -211,7 +223,7 @@ def tile_cheblayer_pb_t_kernel(tc, x, tx1, adj, W, b, out):
 
         def vectors_spread(g):
             v = vectors[g]
-            v["r_cols"] = graph_pool.tile([P, NODES], F32, name="r_cols")
+            v["r_cols"] = graph_pool.tile([P, 2, PASSES, P, 2], F32, name="r_cols")
             for h in range(PASSES):
                 spread = psum_t.tile([P, HALF, P], F32, name="bank")
                 for j in range(HALF):
@@ -220,8 +232,7 @@ def tile_cheblayer_pb_t_kernel(tc, x, tx1, adj, W, b, out):
                         out=spread[:, j, :], in_=v["r"][:, k : k + 1].to_broadcast([P, P]), identity=ident[:]
                     )
                 nc.scalar.copy(
-                    out=v["r_cols"][:, h * K_PASS : (h + 1) * K_PASS].rearrange("p (n t) -> p n t", t=HALF),
-                    in_=spread[:].rearrange("p t n -> p n t"),
+                    out=v["r_cols"][:, :, h], in_=spread[:].rearrange("p (u e) m -> p u m e", e=2)
                 )
 
         chunks = {s: {} for s in range(ALL_CHUNKS + TX2_LAG)}
@@ -231,19 +242,17 @@ def tile_cheblayer_pb_t_kernel(tc, x, tx1, adj, W, b, out):
                 chunks[s]["grouped"] = grouped_pool.tile([P, 4, PASSES, P, PACK], BF16, name="grouped", align_bytes=64)
             return chunks[s]["grouped"]
 
-        def transposed_words(src_half, j):
-            words = src_half[:].bitcast(F32)
+        def transposed_words(planes):
             bank = psum_t.tile([P, PACK, P], F32, name="bank")
-            for a in range(PASSES):
-                for u in range(2):
-                    every_second = words[:, j, 2 * P * a + u : 2 * P * (a + 1) : 2]
-                    nc.tensor.transpose(out=bank[:, 2 * a + u, :], in_=every_second, identity=ident[:])
+            for number, words in enumerate(planes):
+                nc.tensor.transpose(out=bank[:, number, :], in_=words, identity=ident[:])
             return bank
 
         def feat_transpose(s):
             words = grouped_of(s)[:].bitcast(F32)
             for section, name in ((X, "x"), (TX1, "tx1")):
-                bank = transposed_words(half_of(name, s), s % HALF)
+                row = half_of(name, s)[:, s % HALF, :].bitcast(F32).rearrange("p (a m u) -> p a u m", m=P, u=2)
+                bank = transposed_words([row[:, a, u] for a in range(PASSES) for u in range(2)])
                 nc.scalar.copy(out=words[:, section], in_=bank[:].rearrange("p (a u) i -> p a i u", u=2))
 
         def quantise(s, first, last):
@@ -257,18 +266,27 @@ def tile_cheblayer_pb_t_kernel(tc, x, tx1, adj, W, b, out):
                 in_=t["grouped"][:, first:last].rearrange("p m a i t -> p (m a i t)"),
             )
 
+        lap_tiles = {}
+
         def lap_rows(s):
             k = s % CHUNKS
             v = vectors[s // CHUNKS]
-            row = half_of("adj", s)[:, s % HALF, :]
-            nc.vector.scalar_tensor_tensor(
-                out=row, in0=row, scalar=v["neg_r"][:, k : k + 1], in1=v["r_cols"][:], op0=ALU.mult, op1=ALU.mult
-            )
+            lap_tiles[s] = lap_pool.tile([P, 2, PASSES * P, 2], BF16, name="lap")
+            columns = half_of("adj", s)[:, s % HALF, :].rearrange("p (m u e) -> p u m e", u=2, e=2)
+            for u in range(2):
+                nc.vector.scalar_tensor_tensor(
+                    out=lap_tiles[s][:, u],
+                    in0=columns[:, u],
+                    scalar=v["neg_r"][:, k : k + 1],
+                    in1=v["r_cols"][:, u].rearrange("p a m e -> p (a m) e"),
+                    op0=ALU.mult,
+                    op1=ALU.mult,
+                )
 
         def lap_add_eye(s):
             k = s % CHUNKS
-            row = half_of("adj", s)[:, s % HALF, :]
-            diag_cols = row.rearrange("p (h n t) -> p h n t", n=P, t=HALF)[:, k // HALF, :, k % HALF]
+            h, u, e = k // HALF, k % HALF // 2, k % 2
+            diag_cols = lap_tiles[s][:, u, h * P : (h + 1) * P, e]
             nc.vector.scalar_tensor_tensor(
                 out=diag_cols,
                 in0=ident[:],
@@ -279,10 +297,10 @@ def tile_cheblayer_pb_t_kernel(tc, x, tx1, adj, W, b, out):
             )
 
         def lap_transpose(s):
-            bank = transposed_words(half_of("adj", s), s % HALF)
-            pairs = bank[:].bitcast(BF16).rearrange("p (a u) (i e) -> p a i u e", u=2, e=2)
-            for a in range(PASSES):
-                nc.scalar.copy(out=grouped_of(s)[:, LAP, a].rearrange("p i (u e) -> p i u e", e=2), in_=pairs[:, a])
+            row = lap_tiles.pop(s)[:].bitcast(F32).rearrange("p u (a m) o -> p u a (m o)", m=P)
+            bank = transposed_words([row[:, u, a] for a in range(PASSES) for u in range(2)])
+            words = grouped_of(s)[:].bitcast(F32)
+            nc.scalar.copy(out=words[:, LAP], in_=bank[:].rearrange("p (a u) i -> p a i u", u=2))
 
         def second_order_products(s):
             t = chunks[s]
@@ -357,12 +375,7 @@ def tile_cheblayer_pb_t_kernel(tc, x, tx1, adj, W, b, out):
         first_of_graph = lambda s: valid(s) and s % CHUNKS == 0
         second_of_pair = lambda s: valid(s) and s % 2 == 1
 
-        def lap_side(m):
-            if m + EARLY < CHUNKS:
-                return m + EARLY
-            return m if m >= CHUNKS else -1
-
-        first_step = -(AT_ROW_SUMS + LOAD_AHEAD + EARLY)
+        first_step = -(AT_ROW_SUMS + LOAD_AHEAD)
         for n in range(first_step, ALL_CHUNKS - AT_STORE):
             if first_of_half(n + AT_TRANSPOSE + LOAD_AHEAD):
                 load_half("x", x, x_pool, n + AT_TRANSPOSE + LOAD_AHEAD)
@@ -370,43 +383,43 @@ def tile_cheblayer_pb_t_kernel(tc, x, tx1, adj, W, b, out):
                 load_weights()
             if first_of_half(n + AT_NODE_REGROUP + LOAD_AHEAD):
                 load_half("tx1", tx1, tx1_pool, n + AT_NODE_REGROUP + LOAD_AHEAD)
-            if first_of_half(lap_side(n + AT_ROW_SUMS + LOAD_AHEAD)):
-                load_half("adj", adj, adj_pool, lap_side(n + AT_ROW_SUMS + LOAD_AHEAD))
-            if first_of_graph(lap_side(n + AT_ROW_SUMS)):
-                load_diagonal(lap_side(n + AT_ROW_SUMS) // CHUNKS)
+            if first_of_half(n + AT_ROW_SUMS + LOAD_AHEAD):
+                load_half("adj", adj, adj_pool, n + AT_ROW_SUMS + LOAD_AHEAD)
+            if first_of_graph(n + AT_ROW_SUMS):
+                load_diagonal((n + AT_ROW_SUMS) // CHUNKS)
 
-            if first_of_graph(lap_side(n + AT_ROOT)):
-                vectors_root(lap_side(n + AT_ROOT) // CHUNKS)
-            if first_of_graph(lap_side(n + AT_SPREAD)):
-                vectors_spread(lap_side(n + AT_SPREAD) // CHUNKS)
-                vectors_diagonal(lap_side(n + AT_SPREAD) // CHUNKS)
+            if first_of_graph(n + AT_ROOT):
+                vectors_root((n + AT_ROOT) // CHUNKS)
+            if first_of_graph(n + AT_SPREAD):
+                vectors_spread((n + AT_SPREAD) // CHUNKS)
+                vectors_diagonal((n + AT_SPREAD) // CHUNKS)
 
             if second_of_pair(n + AT_RELU):
                 output_relu(n + AT_RELU)
-            if valid(n + AT_NODE_REGROUP):
-                node_regroup(n + AT_NODE_REGROUP)
 
             if valid(n + AT_OUTPUT):
                 output_products(n + AT_OUTPUT)
-            if valid(lap_side(n + AT_ROW_SUMS)):
-                row_sums(lap_side(n + AT_ROW_SUMS))
-            if second_of_pair(n + AT_STORE):
-                output_store(n + AT_STORE)
+            if valid(n + AT_ROW_SUMS):
+                row_sums(n + AT_ROW_SUMS)
             if valid(n + AT_TRANSPOSE):
                 feat_transpose(n + AT_TRANSPOSE)
                 lap_transpose(n + AT_TRANSPOSE)
+            if valid(n + AT_NODE_REGROUP):
+                node_regroup(n + AT_NODE_REGROUP)
+            if second_of_pair(n + AT_STORE):
+                output_store(n + AT_STORE)
 
             if n + AT_QUANTISE == 0:
                 quantise_weights()
-            if first_of_graph(lap_side(n + AT_RECIPROCAL)):
-                vectors_reciprocal(lap_side(n + AT_RECIPROCAL) // CHUNKS)
-            if valid(lap_side(n + AT_LAP)):
-                lap_rows(lap_side(n + AT_LAP))
+            if first_of_graph(n + AT_RECIPROCAL):
+                vectors_reciprocal((n + AT_RECIPROCAL) // CHUNKS)
+            if valid(n + AT_LAP):
+                lap_rows(n + AT_LAP)
             if valid(n + AT_TERM):
                 second_order_term(n + AT_TERM, 0)
                 second_order_term(n + AT_TERM, 1)
-            if valid(lap_side(n + AT_LAP)):
-                lap_add_eye(lap_side(n + AT_LAP))
+            if valid(n + AT_LAP):
+                lap_add_eye(n + AT_LAP)
             if valid(n + AT_QUANTISE) and valid(n + AT_TERM):
                 quantise(n + AT_QUANTISE, X, TX2 + 1)
             elif valid(n + AT_QUANTISE):

@@ -129,15 +129,16 @@ def tile_cheblayer_pb_t_kernel(tc, x, tx1, adj, W, b, out):
         node_grouped = {}
 
         def node_regroup(q):
-            if q % 2 == 0:
-                node_grouped[q // 2] = short.tile([P, 2, 2, P, PACK], BF16, name="node_grouped", align_bytes=64)
-            j = q % HALF
-            features = half_of("tx1", q)[:, :, (j // 2) * K_PASS : (j // 2 + 1) * K_PASS]
-            rows = features.rearrange("p t (m v) -> p v m t", v=PACK)[:, 2 * (j % 2) : 2 * (j % 2) + 2]
+            j, w = q % HALF, q % 2
+            if w == 0:
+                node_grouped[q // 2] = short.tile([P, PACK, P, PACK], BF16, name="node_grouped", align_bytes=64)
+            words = slice(w * P // 2, (w + 1) * P // 2)
+            grouped = node_grouped[q // 2][:, :, words, :].rearrange("p v m t -> p m t v")
+            rows = half_of("tx1", q)[:, :, j * 2 * P : (j + 1) * 2 * P].rearrange("p t (m v) -> p m t v", v=PACK)
             if q < CHUNKS:
-                nc.vector.tensor_copy(out=node_grouped[q // 2][:, q % 2], in_=rows)
+                nc.vector.tensor_copy(out=grouped, in_=rows)
             else:
-                nc.scalar.copy(out=node_grouped[q // 2][:, q % 2], in_=rows)
+                nc.scalar.copy(out=grouped, in_=rows)
 
         def node_quantise(q):
             key = (q // CHUNKS, (q % CHUNKS) // HALF)
@@ -151,7 +152,7 @@ def tile_cheblayer_pb_t_kernel(tc, x, tx1, adj, W, b, out):
             nc.vector.quantize_mx(
                 out=codes[:, windows].bitcast(FP8X4),
                 scales=scales[:, windows],
-                in_=node_grouped[q // 2][:].rearrange("p w e m t -> p (w e m t)"),
+                in_=node_grouped[q // 2][:].rearrange("p v m t -> p (v m t)"),
             )
 
         def row_sums(q):

@@ -39,7 +39,7 @@ AT_SPREAD = AT_LAP + 1
 AT_RECIPROCAL = AT_LAP + 2
 AT_ROOT = AT_LAP + 3
 AT_ROW_SUMS = AT_ROOT + CHUNKS
-AT_NODE_QUANTISE = AT_SECOND_ORDER + 1 + CHUNKS
+AT_NODE_QUANTISE = AT_SECOND_ORDER + CHUNKS
 AT_NODE_REGROUP = AT_NODE_QUANTISE + 1
 X, TX1, LAP, TX2 = 0, 1, 2, 3
 TX2_LAG = AT_QUANTISE - AT_TERM
@@ -161,7 +161,7 @@ def tile_cheblayer_pb_t_kernel(tc, x, tx1, adj, W, b, out):
                 vectors[g]["d"] = graph_pool.tile([P, CHUNKS], F32, name="d")
             d = vectors[g]["d"][:, k : k + 1]
             row = half_of("adj", q)[:, q % HALF, :]
-            if g == 0 and k % 2 == 0:
+            if g == 0 and k in (0, 1, 6, 7):
                 junk = short.tile([P, NODES], BF16, name="junk_row")
                 nc.vector.tensor_scalar(
                     out=junk[:], in0=row, scalar1=1.0, scalar2=None, op0=ALU.mult, op1=ALU.add, accum_out=d
@@ -269,33 +269,43 @@ def tile_cheblayer_pb_t_kernel(tc, x, tx1, adj, W, b, out):
 
         lap_tiles = {}
 
-        def lap_rows(s):
+        def diagonal_plane(s):
+            return s % HALF // 2
+
+        def lap_rows(s, u):
             k = s % CHUNKS
             v = vectors[s // CHUNKS]
-            lap_tiles[s] = lap_pool.tile([P, 2, PASSES * P, 2], BF16, name="lap")
+            if s not in lap_tiles:
+                lap_tiles[s] = lap_pool.tile([P, 2, PASSES * P, 2], BF16, name="lap")
             columns = half_of("adj", s)[:, s % HALF, :].rearrange("p (m u e) -> p u m e", u=2, e=2)
-            for u in range(2):
-                nc.vector.scalar_tensor_tensor(
-                    out=lap_tiles[s][:, u],
-                    in0=columns[:, u],
-                    scalar=v["neg_r"][:, k : k + 1],
-                    in1=v["r_cols"][:, u].rearrange("p a m e -> p (a m) e"),
-                    op0=ALU.mult,
-                    op1=ALU.mult,
-                )
-
-        def lap_add_eye(s):
-            k = s % CHUNKS
-            h, u, e = k // HALF, k % HALF // 2, k % 2
-            diag_cols = lap_tiles[s][:, u, h * P : (h + 1) * P, e]
             nc.vector.scalar_tensor_tensor(
-                out=diag_cols,
+                out=lap_tiles[s][:, u],
+                in0=columns[:, u],
+                scalar=v["neg_r"][:, k : k + 1],
+                in1=v["r_cols"][:, u].rearrange("p a m e -> p (a m) e"),
+                op0=ALU.mult,
+                op1=ALU.mult,
+            )
+
+        eye_rows = {}
+
+        def lap_eye_row(s):
+            eye_rows[s] = short.tile([P, P], F32, name="eye_row")
+            k = s % CHUNKS
+            nc.gpsimd.tensor_scalar(
+                out=eye_rows[s][:],
                 in0=ident[:],
-                scalar=vectors[s // CHUNKS]["eye_fix"][:, k : k + 1],
-                in1=diag_cols,
+                scalar1=vectors[s // CHUNKS]["eye_fix"][:, k : k + 1],
+                scalar2=0.0,
                 op0=ALU.mult,
                 op1=ALU.add,
             )
+
+        def lap_add_eye(s):
+            k = s % CHUNKS
+            h = k // HALF
+            diag_cols = lap_tiles[s][:, diagonal_plane(s), h * P : (h + 1) * P, k % 2]
+            nc.gpsimd.tensor_tensor(out=diag_cols, in0=eye_rows.pop(s)[:], in1=diag_cols, op=ALU.add)
 
         def lap_transpose(s):
             row = lap_tiles.pop(s)[:].bitcast(F32).rearrange("p u (a m) o -> p u a (m o)", m=P)
@@ -377,14 +387,17 @@ def tile_cheblayer_pb_t_kernel(tc, x, tx1, adj, W, b, out):
         second_of_pair = lambda s: valid(s) and s % 2 == 1
 
         first_step = -(AT_ROW_SUMS + LOAD_AHEAD)
+        for q in range(0, CHUNKS, HALF):
+            load_half("adj", adj, adj_pool, q)
+            load_half("tx1", tx1, tx1_pool, q)
         for n in range(first_step, ALL_CHUNKS - AT_STORE):
             if first_of_half(n + AT_TRANSPOSE + LOAD_AHEAD):
                 load_half("x", x, x_pool, n + AT_TRANSPOSE + LOAD_AHEAD)
             if n + AT_TRANSPOSE + LOAD_AHEAD == 0:
                 load_weights()
-            if first_of_half(n + AT_NODE_REGROUP + LOAD_AHEAD):
+            if first_of_half(n + AT_NODE_REGROUP + LOAD_AHEAD) and n + AT_NODE_REGROUP + LOAD_AHEAD >= CHUNKS:
                 load_half("tx1", tx1, tx1_pool, n + AT_NODE_REGROUP + LOAD_AHEAD)
-            if first_of_half(n + AT_ROW_SUMS + LOAD_AHEAD):
+            if first_of_half(n + AT_ROW_SUMS + LOAD_AHEAD) and n + AT_ROW_SUMS + LOAD_AHEAD >= CHUNKS:
                 load_half("adj", adj, adj_pool, n + AT_ROW_SUMS + LOAD_AHEAD)
             if first_of_graph(n + AT_ROW_SUMS):
                 load_diagonal((n + AT_ROW_SUMS) // CHUNKS)
@@ -405,7 +418,7 @@ def tile_cheblayer_pb_t_kernel(tc, x, tx1, adj, W, b, out):
             if valid(n + AT_TRANSPOSE):
                 feat_transpose(n + AT_TRANSPOSE)
                 lap_transpose(n + AT_TRANSPOSE)
-            if valid(n + AT_NODE_REGROUP):
+            if valid(n + AT_NODE_REGROUP) and n + AT_NODE_REGROUP >= CHUNKS:
                 node_regroup(n + AT_NODE_REGROUP)
             if second_of_pair(n + AT_STORE):
                 output_store(n + AT_STORE)
@@ -414,13 +427,18 @@ def tile_cheblayer_pb_t_kernel(tc, x, tx1, adj, W, b, out):
                 quantise_weights()
             if first_of_graph(n + AT_RECIPROCAL):
                 vectors_reciprocal((n + AT_RECIPROCAL) // CHUNKS)
+            if valid(n + AT_NODE_REGROUP) and n + AT_NODE_REGROUP < CHUNKS:
+                node_regroup(n + AT_NODE_REGROUP)
             if valid(n + AT_LAP):
-                lap_rows(n + AT_LAP)
+                lap_rows(n + AT_LAP, diagonal_plane(n + AT_LAP))
+                lap_add_eye(n + AT_LAP)
+            if valid(n + AT_LAP + 1):
+                lap_eye_row(n + AT_LAP + 1)
             if valid(n + AT_TERM):
                 second_order_term(n + AT_TERM, 0)
                 second_order_term(n + AT_TERM, 1)
             if valid(n + AT_LAP):
-                lap_add_eye(n + AT_LAP)
+                lap_rows(n + AT_LAP, 1 - diagonal_plane(n + AT_LAP))
             if valid(n + AT_QUANTISE) and valid(n + AT_TERM):
                 quantise(n + AT_QUANTISE, X, TX2 + 1)
             elif valid(n + AT_QUANTISE):

@@ -36,14 +36,14 @@ AT_QUANTISE = 4
 AT_TRANSPOSE = 5
 AT_LAP = 6
 AT_SPREAD = AT_LAP + 1
-AT_RECIPROCAL = AT_LAP + 2
-AT_ROOT = AT_LAP + 3
-AT_ROW_SUMS = AT_ROOT + CHUNKS
+AT_R = AT_LAP + 2
+AT_ROW_SUMS = AT_R + CHUNKS
 AT_NODE_QUANTISE = AT_SECOND_ORDER + CHUNKS
 AT_NODE_REGROUP = AT_NODE_QUANTISE + 1
 X, TX1, LAP, TX2 = 0, 1, 2, 3
 TX2_LAG = AT_QUANTISE - AT_TERM
 LOAD_AHEAD = 4
+FEATS_EARLY = 2
 ADJ_BUFS = 5
 LAP_BUFS = AT_LAP - AT_TRANSPOSE + 1
 TX1_BUFS = 4
@@ -81,7 +81,7 @@ def tile_cheblayer_pb_t_kernel(tc, x, tx1, adj, W, b, out):
         eps = const.tile([P, 1], F32)
         nc.vector.memset(eps[:], EPS)
         warm = const.tile([P, 1], F32)
-        nc.scalar.activation(out=warm[:], in_=eps[:], func=ACT.Sqrt)
+        nc.scalar.activation(out=warm[:], in_=eps[:], func=ACT.Abs_reciprocal_sqrt)
 
         halves = {}
 
@@ -161,12 +161,12 @@ def tile_cheblayer_pb_t_kernel(tc, x, tx1, adj, W, b, out):
                 vectors[g]["d"] = graph_pool.tile([P, CHUNKS], F32, name="d")
             d = vectors[g]["d"][:, k : k + 1]
             row = half_of("adj", q)[:, q % HALF, :]
-            if g == 0 and k in (0, 1, 6, 7):
+            if k == 7:
                 junk = short.tile([P, NODES], BF16, name="junk_row")
                 nc.vector.tensor_scalar(
                     out=junk[:], in0=row, scalar1=1.0, scalar2=None, op0=ALU.mult, op1=ALU.add, accum_out=d
                 )
-            elif g == 0 or k % 2 == 0:
+            elif k in (0, 4) or g == 0 and k in (2, 6):
                 junk = short.tile([P, NODES], BF16, name="junk_row")
                 nc.scalar.activation(out=junk[:], in_=row, func=ACT.Copy, accum_out=d)
             else:
@@ -182,16 +182,11 @@ def tile_cheblayer_pb_t_kernel(tc, x, tx1, adj, W, b, out):
                 junk = short.tile([P, P], F32, name="junk")
                 nc.scalar.activation(out=junk[:], in_=folded[:], func=ACT.Copy, accum_out=d)
 
-        def vectors_root(g):
-            vectors[g]["root"] = graph_pool.tile([P, CHUNKS], F32, name="root")
-            nc.scalar.activation(out=vectors[g]["root"][:], in_=vectors[g]["d"][:], func=ACT.Sqrt, bias=eps[:, 0:1])
-
-        def vectors_reciprocal(g):
-            v = vectors[g]
-            v["r"] = graph_pool.tile([P, CHUNKS], F32, name="r")
-            nc.vector.reciprocal(out=v["r"][:], in_=v["root"][:])
-            v["neg_r"] = graph_pool.tile([P, CHUNKS], F32, name="neg_r")
-            nc.vector.tensor_scalar_mul(out=v["neg_r"][:], in0=v["r"][:], scalar1=-1.0)
+        def vectors_r(g):
+            vectors[g]["r"] = graph_pool.tile([P, CHUNKS], F32, name="r")
+            nc.scalar.activation(
+                out=vectors[g]["r"][:], in_=vectors[g]["d"][:], func=ACT.Abs_reciprocal_sqrt, bias=eps[:, 0:1]
+            )
 
         def load_diagonal(g):
             vectors[g]["a_diag"] = graph_pool.tile([P, 2, BLOCK_BF16], BF16, name="a_diag")
@@ -206,25 +201,27 @@ def tile_cheblayer_pb_t_kernel(tc, x, tx1, adj, W, b, out):
         def vectors_diagonal(g):
             v = vectors[g]
             small = lambda name, dtype: graph_pool.tile([P, CHUNKS], dtype, name=name)
-            half_product, product, stored, one_more = (
-                small("half_product", F32), small("product", F32), small("stored", BF16), small("one_more", F32)
+            half_product, product, stored, one_less = (
+                small("half_product", F32), small("product", F32), small("stored", BF16), small("one_less", F32)
             )
             v["eye_fix"] = small("eye_fix", F32)
             by_half = lambda ap: ap.rearrange("p (h t) -> p h t", t=HALF)
             nc.gpsimd.tensor_tensor(
                 out=by_half(half_product[:]),
                 in0=v["a_diag"][:, :, 0:HALF],
-                in1=by_half(v["neg_r"][:]),
+                in1=by_half(v["r"][:]),
                 op=ALU.mult,
             )
             nc.gpsimd.tensor_tensor(out=product[:], in0=half_product[:], in1=v["r"][:], op=ALU.mult)
             nc.gpsimd.tensor_copy(out=stored[:], in_=product[:])
-            nc.gpsimd.tensor_scalar_add(out=one_more[:], in0=product[:], scalar1=1.0)
-            nc.gpsimd.tensor_tensor(out=v["eye_fix"][:], in0=one_more[:], in1=stored[:], op=ALU.subtract)
+            nc.gpsimd.tensor_scalar(
+                out=one_less[:], in0=product[:], scalar1=-1.0, scalar2=1.0, op0=ALU.mult, op1=ALU.add
+            )
+            nc.gpsimd.tensor_tensor(out=v["eye_fix"][:], in0=one_less[:], in1=stored[:], op=ALU.add)
 
         def vectors_spread(g):
             v = vectors[g]
-            v["r_cols"] = graph_pool.tile([P, 2, PASSES, P, 2], F32, name="r_cols")
+            v["neg_r_cols"] = graph_pool.tile([P, 2, PASSES, P, 2], F32, name="neg_r_cols")
             for h in range(PASSES):
                 spread = psum_t.tile([P, HALF, P], F32, name="bank")
                 for j in range(HALF):
@@ -232,8 +229,11 @@ def tile_cheblayer_pb_t_kernel(tc, x, tx1, adj, W, b, out):
                     nc.tensor.transpose(
                         out=spread[:, j, :], in_=v["r"][:, k : k + 1].to_broadcast([P, P]), identity=ident[:]
                     )
-                nc.scalar.copy(
-                    out=v["r_cols"][:, :, h], in_=spread[:].rearrange("p (u e) m -> p u m e", e=2)
+                nc.scalar.activation(
+                    out=v["neg_r_cols"][:, :, h],
+                    in_=spread[:].rearrange("p (u e) m -> p u m e", e=2),
+                    func=ACT.Copy,
+                    scale=-1.0,
                 )
 
         chunks = {s: {} for s in range(ALL_CHUNKS + TX2_LAG)}
@@ -281,8 +281,8 @@ def tile_cheblayer_pb_t_kernel(tc, x, tx1, adj, W, b, out):
             nc.vector.scalar_tensor_tensor(
                 out=lap_tiles[s][:, u],
                 in0=columns[:, u],
-                scalar=v["neg_r"][:, k : k + 1],
-                in1=v["r_cols"][:, u].rearrange("p a m e -> p (a m) e"),
+                scalar=v["r"][:, k : k + 1],
+                in1=v["neg_r_cols"][:, u].rearrange("p a m e -> p (a m) e"),
                 op0=ALU.mult,
                 op1=ALU.mult,
             )
@@ -382,29 +382,48 @@ def tile_cheblayer_pb_t_kernel(tc, x, tx1, adj, W, b, out):
             nc.sync.dma_start(out=rows[:, t : t + 2, :], in_=result[:])
 
         valid = lambda s: 0 <= s < ALL_CHUNKS
+        later_graph = lambda s: CHUNKS <= s < ALL_CHUNKS
         first_of_half = lambda s: valid(s) and s % HALF == 0
         first_of_graph = lambda s: valid(s) and s % CHUNKS == 0
         second_of_pair = lambda s: valid(s) and s % 2 == 1
 
-        first_step = -(AT_ROW_SUMS + LOAD_AHEAD)
-        for q in range(0, CHUNKS, HALF):
-            load_half("adj", adj, adj_pool, q)
-            load_half("tx1", tx1, tx1_pool, q)
+        first_step = -(AT_ROW_SUMS + LOAD_AHEAD - CHUNKS)
+        load_half("tx1", tx1, tx1_pool, 0)
+        load_half("adj", adj, adj_pool, 0)
+        load_half("tx1", tx1, tx1_pool, HALF)
+        load_half("adj", adj, adj_pool, HALF)
+        load_diagonal(0)
+        load_half("x", x, x_pool, 0)
+        load_weights()
+        for q in range(HALF):
+            node_regroup(q)
+            row_sums(q)
+            if q % 2 == 1:
+                node_quantise(q)
+        for q in range(HALF, CHUNKS):
+            node_regroup(q)
+            row_sums(q)
+            if q % 2 == 1:
+                node_quantise(q)
+        vectors_r(0)
+        vectors_spread(0)
+        vectors_diagonal(0)
+        for s in range(FEATS_EARLY):
+            feat_transpose(s)
+        quantise_weights()
         for n in range(first_step, ALL_CHUNKS - AT_STORE):
-            if first_of_half(n + AT_TRANSPOSE + LOAD_AHEAD):
+            if first_of_half(n + AT_TRANSPOSE + LOAD_AHEAD) and n + AT_TRANSPOSE + LOAD_AHEAD > 0:
                 load_half("x", x, x_pool, n + AT_TRANSPOSE + LOAD_AHEAD)
-            if n + AT_TRANSPOSE + LOAD_AHEAD == 0:
-                load_weights()
-            if first_of_half(n + AT_NODE_REGROUP + LOAD_AHEAD) and n + AT_NODE_REGROUP + LOAD_AHEAD >= CHUNKS:
+            if later_graph(n + AT_NODE_REGROUP + LOAD_AHEAD) and first_of_half(n + AT_NODE_REGROUP + LOAD_AHEAD):
                 load_half("tx1", tx1, tx1_pool, n + AT_NODE_REGROUP + LOAD_AHEAD)
-            if first_of_half(n + AT_ROW_SUMS + LOAD_AHEAD) and n + AT_ROW_SUMS + LOAD_AHEAD >= CHUNKS:
+            if later_graph(n + AT_ROW_SUMS + LOAD_AHEAD) and first_of_half(n + AT_ROW_SUMS + LOAD_AHEAD):
                 load_half("adj", adj, adj_pool, n + AT_ROW_SUMS + LOAD_AHEAD)
-            if first_of_graph(n + AT_ROW_SUMS):
+            if later_graph(n + AT_ROW_SUMS) and first_of_graph(n + AT_ROW_SUMS):
                 load_diagonal((n + AT_ROW_SUMS) // CHUNKS)
 
-            if first_of_graph(n + AT_ROOT):
-                vectors_root((n + AT_ROOT) // CHUNKS)
-            if first_of_graph(n + AT_SPREAD):
+            if later_graph(n + AT_R) and first_of_graph(n + AT_R):
+                vectors_r((n + AT_R) // CHUNKS)
+            if later_graph(n + AT_SPREAD) and first_of_graph(n + AT_SPREAD):
                 vectors_spread((n + AT_SPREAD) // CHUNKS)
                 vectors_diagonal((n + AT_SPREAD) // CHUNKS)
 
@@ -413,22 +432,17 @@ def tile_cheblayer_pb_t_kernel(tc, x, tx1, adj, W, b, out):
 
             if valid(n + AT_OUTPUT):
                 output_products(n + AT_OUTPUT)
-            if valid(n + AT_ROW_SUMS):
+            if later_graph(n + AT_ROW_SUMS):
                 row_sums(n + AT_ROW_SUMS)
             if valid(n + AT_TRANSPOSE):
-                feat_transpose(n + AT_TRANSPOSE)
+                if n + AT_TRANSPOSE >= FEATS_EARLY:
+                    feat_transpose(n + AT_TRANSPOSE)
                 lap_transpose(n + AT_TRANSPOSE)
-            if valid(n + AT_NODE_REGROUP) and n + AT_NODE_REGROUP >= CHUNKS:
+            if later_graph(n + AT_NODE_REGROUP):
                 node_regroup(n + AT_NODE_REGROUP)
             if second_of_pair(n + AT_STORE):
                 output_store(n + AT_STORE)
 
-            if n + AT_QUANTISE == 0:
-                quantise_weights()
-            if first_of_graph(n + AT_RECIPROCAL):
-                vectors_reciprocal((n + AT_RECIPROCAL) // CHUNKS)
-            if valid(n + AT_NODE_REGROUP) and n + AT_NODE_REGROUP < CHUNKS:
-                node_regroup(n + AT_NODE_REGROUP)
             if valid(n + AT_LAP):
                 lap_rows(n + AT_LAP, diagonal_plane(n + AT_LAP))
                 lap_add_eye(n + AT_LAP)
@@ -446,7 +460,7 @@ def tile_cheblayer_pb_t_kernel(tc, x, tx1, adj, W, b, out):
                 quantise(n + AT_QUANTISE, LAP, LAP + 1)
             elif valid(n + AT_TERM):
                 quantise(n + AT_QUANTISE, TX2, TX2 + 1)
-            if second_of_pair(n + AT_NODE_QUANTISE):
+            if later_graph(n + AT_NODE_QUANTISE) and second_of_pair(n + AT_NODE_QUANTISE):
                 node_quantise(n + AT_NODE_QUANTISE)
 
             if valid(n + AT_SECOND_ORDER):

@@ -161,12 +161,12 @@ def tile_cheblayer_pb_t_kernel(tc, x, tx1, adj, W, b, out):
                 vectors[g]["d"] = graph_pool.tile([P, CHUNKS], F32, name="d")
             d = vectors[g]["d"][:, k : k + 1]
             row = half_of("adj", q)[:, q % HALF, :]
-            if k == 7:
+            if g == 0 and k == 7:
                 junk = short.tile([P, NODES], BF16, name="junk_row")
                 nc.vector.tensor_scalar(
                     out=junk[:], in0=row, scalar1=1.0, scalar2=None, op0=ALU.mult, op1=ALU.add, accum_out=d
                 )
-            elif k in (0, 4) or g == 0 and k in (2, 6):
+            elif k % 2 == 0:
                 junk = short.tile([P, NODES], BF16, name="junk_row")
                 nc.scalar.activation(out=junk[:], in_=row, func=ACT.Copy, accum_out=d)
             else:
@@ -297,6 +297,19 @@ def tile_cheblayer_pb_t_kernel(tc, x, tx1, adj, W, b, out):
                 in0=ident[:],
                 scalar1=vectors[s // CHUNKS]["eye_fix"][:, k : k + 1],
                 scalar2=0.0,
+                op0=ALU.mult,
+                op1=ALU.add,
+            )
+
+        def lap_add_eye_vector(s):
+            k = s % CHUNKS
+            h = k // HALF
+            diag_cols = lap_tiles[s][:, diagonal_plane(s), h * P : (h + 1) * P, k % 2]
+            nc.vector.scalar_tensor_tensor(
+                out=diag_cols,
+                in0=ident[:],
+                scalar=vectors[s // CHUNKS]["eye_fix"][:, k : k + 1],
+                in1=diag_cols,
                 op0=ALU.mult,
                 op1=ALU.add,
             )
@@ -445,14 +458,17 @@ def tile_cheblayer_pb_t_kernel(tc, x, tx1, adj, W, b, out):
 
             if valid(n + AT_LAP):
                 lap_rows(n + AT_LAP, diagonal_plane(n + AT_LAP))
-                lap_add_eye(n + AT_LAP)
-            if valid(n + AT_LAP + 1):
+                if valid(n + AT_TERM):
+                    lap_add_eye(n + AT_LAP)
+            if valid(n + AT_LAP + 1) and valid(n + AT_TERM + 1):
                 lap_eye_row(n + AT_LAP + 1)
             if valid(n + AT_TERM):
                 second_order_term(n + AT_TERM, 0)
                 second_order_term(n + AT_TERM, 1)
             if valid(n + AT_LAP):
                 lap_rows(n + AT_LAP, 1 - diagonal_plane(n + AT_LAP))
+                if not valid(n + AT_TERM):
+                    lap_add_eye_vector(n + AT_LAP)
             if valid(n + AT_QUANTISE) and valid(n + AT_TERM):
                 quantise(n + AT_QUANTISE, X, TX2 + 1)
             elif valid(n + AT_QUANTISE):

@@ -43,7 +43,7 @@ AT_NODE_REGROUP = AT_NODE_QUANTISE + 1
 X, TX1, LAP, TX2 = 0, 1, 2, 3
 TX2_LAG = AT_QUANTISE - AT_TERM
 LOAD_AHEAD = 4
-FEATS_EARLY = 2
+FEATS_EARLY = 1
 ADJ_BUFS = 5
 LAP_BUFS = AT_LAP - AT_TRANSPOSE + 1
 TX1_BUFS = 4
@@ -67,6 +67,7 @@ def tile_cheblayer_pb_t_kernel(tc, x, tx1, adj, W, b, out):
         node_pool = pool("node", 5)
         short = pool("short", 3)
         lap_pool = pool("lap", LAP_BUFS)
+        sorted_pool = pool("sorted", 2)
         grouped_pool = pool("grouped", 5)
         codes_pool = pool("codes", 4)
         psum_t = stack.enter_context(tc.psum_pool(name="psum_t", bufs=4))
@@ -96,12 +97,13 @@ def tile_cheblayer_pb_t_kernel(tc, x, tx1, adj, W, b, out):
         def half_of(name, s):
             return halves[(name, s // CHUNKS, (s % CHUNKS) // HALF)]
 
-        w_raw = const.tile([P, ORDERS * PASSES, PACK, OUT], BF16)
-        w_grouped = const.tile([P, ORDERS * PASSES, OUT, PACK], BF16, align_bytes=64)
+        w_raw = grouped_pool.tile([P, ORDERS * PASSES, PACK, OUT], BF16, name="grouped", align_bytes=64)
+        w_grouped = grouped_pool.tile([P, ORDERS * PASSES, OUT, PACK], BF16, name="grouped", align_bytes=64)
         w_codes = const.tile([P, ORDERS, PASSES, OUT], U32, align_bytes=64)
         w_scales = const.tile([P, ORDERS, PASSES, OUT], U8, align_bytes=64)
         b_rows = const.tile([P, P], BF16)
         b_terms = const.tile([P, ORDERS], F32)
+        bias_row = const.tile([P, OUT], F32)
         bias = const.tile([P, 1], F32)
 
         def load_weights():
@@ -123,6 +125,9 @@ def tile_cheblayer_pb_t_kernel(tc, x, tx1, adj, W, b, out):
             b_cols = psum_t.tile([P, P], BF16, name="bank")
             nc.tensor.transpose(out=b_cols[:], in_=b_rows[:], identity=ident_bf[:])
             nc.scalar.activation(out=b_terms[:], in_=b_cols[:, 0:ORDERS], func=ACT.Copy, accum_out=bias[:, 0:1])
+            b_spread = psum_t.tile([P, OUT], F32, name="bank")
+            nc.tensor.transpose(out=b_spread[:], in_=bias[:, 0:1].to_broadcast([P, OUT]), identity=ident[:])
+            nc.scalar.copy(out=bias_row[:], in_=b_spread[:])
 
         vectors = {g: {} for g in range(GRAPHS)}
         node_codes = {}
@@ -161,12 +166,7 @@ def tile_cheblayer_pb_t_kernel(tc, x, tx1, adj, W, b, out):
                 vectors[g]["d"] = graph_pool.tile([P, CHUNKS], F32, name="d")
             d = vectors[g]["d"][:, k : k + 1]
             row = half_of("adj", q)[:, q % HALF, :]
-            if g == 0 and k == 7:
-                junk = short.tile([P, NODES], BF16, name="junk_row")
-                nc.vector.tensor_scalar(
-                    out=junk[:], in0=row, scalar1=1.0, scalar2=None, op0=ALU.mult, op1=ALU.add, accum_out=d
-                )
-            elif k % 2 == 0:
+            if k % 2 == 0:
                 junk = short.tile([P, NODES], BF16, name="junk_row")
                 nc.scalar.activation(out=junk[:], in_=row, func=ACT.Copy, accum_out=d)
             else:
@@ -249,11 +249,21 @@ def tile_cheblayer_pb_t_kernel(tc, x, tx1, adj, W, b, out):
                 nc.tensor.transpose(out=bank[:, number, :], in_=words, identity=ident[:])
             return bank
 
+        sorted_rows = {}
+
+        def words_of(name, s):
+            return half_of(name, s)[:, s % HALF, :].bitcast(F32).rearrange("p (w u) -> p u w", u=2)
+
+        def feat_sort(s):
+            sorted_rows[s] = sorted_pool.tile([P, 2, 2, PASSES * P], F32, name="sorted")
+            for section, name in ((X, "x"), (TX1, "tx1")):
+                nc.scalar.copy(out=sorted_rows[s][:, section], in_=words_of(name, s))
+
         def feat_transpose(s):
             words = grouped_of(s)[:].bitcast(F32)
             for section, name in ((X, "x"), (TX1, "tx1")):
-                row = half_of(name, s)[:, s % HALF, :].bitcast(F32).rearrange("p (a m u) -> p a u m", m=P, u=2)
-                bank = transposed_words([row[:, a, u] for a in range(PASSES) for u in range(2)])
+                row = sorted_rows[s][:, section] if s in sorted_rows else words_of(name, s)
+                bank = transposed_words([row[:, u, a * P : (a + 1) * P] for a in range(PASSES) for u in range(2)])
                 nc.scalar.copy(out=words[:, section], in_=bank[:].rearrange("p (a u) i -> p a i u", u=2))
 
         def quantise(s, first, last):
@@ -358,6 +368,37 @@ def tile_cheblayer_pb_t_kernel(tc, x, tx1, adj, W, b, out):
 
         pair_acc = {}
 
+        def output_products_direct(s):
+            t, later = chunks[s], chunks[s + TX2_LAG]
+            if s % 2 == 0:
+                pair_acc[s // 2] = psum_o.tile([P, 2, P], F32, name="out_acc")
+            acc = pair_acc[s // 2][:, s % 2, :]
+            operands = [
+                (t["codes"][:, X], t["scales"][:, X]),
+                (t["codes"][:, TX1], t["scales"][:, TX1]),
+                (later["codes"][:, TX2], later["scales"][:, TX2]),
+            ]
+            for k, (codes, scales) in enumerate(operands):
+                for a in range(PASSES):
+                    nc.tensor.matmul_mx(
+                        out=acc,
+                        lhsT=codes[:, a, :].bitcast(FP8X4),
+                        lhsT_scale=scales[:, a, :],
+                        rhs=w_codes[:, k, a, :].bitcast(FP8X4),
+                        rhs_scale=w_scales[:, k, a, :],
+                        start=(k == 0 and a == 0),
+                        stop=(k == ORDERS - 1 and a == PASSES - 1),
+                    )
+
+        def output_relu_direct(s):
+            total = short.tile([P, OUT], F32, name="total")
+            nc.vector.tensor_tensor(out=total[:], in0=pair_acc[s // 2][:, s % 2, :], in1=bias_row[:], op=ALU.add)
+            result = short.tile([P, OUT], F32, name="result_direct")
+            nc.vector.tensor_scalar_max(out=result[:], in0=total[:], scalar1=0.0)
+            g, h = s // CHUNKS, (s % CHUNKS) // HALF
+            rows = out[g, h * K_PASS : (h + 1) * K_PASS, :].rearrange("(p t) o -> p t o", t=HALF)
+            nc.sync.dma_start(out=rows[:, s % HALF, :], in_=result[:])
+
         def output_products(s):
             t = chunks[s]
             if s % 2 == 0:
@@ -395,6 +436,8 @@ def tile_cheblayer_pb_t_kernel(tc, x, tx1, adj, W, b, out):
             nc.sync.dma_start(out=rows[:, t : t + 2, :], in_=result[:])
 
         valid = lambda s: 0 <= s < ALL_CHUNKS
+        last_pair = lambda s: ALL_CHUNKS - 2 <= s < ALL_CHUNKS
+        last_graph = lambda s: ALL_CHUNKS - CHUNKS <= s < ALL_CHUNKS
         later_graph = lambda s: CHUNKS <= s < ALL_CHUNKS
         first_of_half = lambda s: valid(s) and s % HALF == 0
         first_of_graph = lambda s: valid(s) and s % CHUNKS == 0
@@ -406,8 +449,8 @@ def tile_cheblayer_pb_t_kernel(tc, x, tx1, adj, W, b, out):
         load_half("tx1", tx1, tx1_pool, HALF)
         load_half("adj", adj, adj_pool, HALF)
         load_diagonal(0)
-        load_half("x", x, x_pool, 0)
         load_weights()
+        load_half("x", x, x_pool, 0)
         for q in range(HALF):
             node_regroup(q)
             row_sums(q)
@@ -440,10 +483,12 @@ def tile_cheblayer_pb_t_kernel(tc, x, tx1, adj, W, b, out):
                 vectors_spread((n + AT_SPREAD) // CHUNKS)
                 vectors_diagonal((n + AT_SPREAD) // CHUNKS)
 
-            if second_of_pair(n + AT_RELU):
+            if second_of_pair(n + AT_RELU) and not last_pair(n + AT_RELU):
                 output_relu(n + AT_RELU)
 
-            if valid(n + AT_OUTPUT):
+            if last_pair(n + AT_OUTPUT):
+                output_products_direct(n + AT_OUTPUT)
+            elif valid(n + AT_OUTPUT):
                 output_products(n + AT_OUTPUT)
             if later_graph(n + AT_ROW_SUMS):
                 row_sums(n + AT_ROW_SUMS)
@@ -451,9 +496,11 @@ def tile_cheblayer_pb_t_kernel(tc, x, tx1, adj, W, b, out):
                 if n + AT_TRANSPOSE >= FEATS_EARLY:
                     feat_transpose(n + AT_TRANSPOSE)
                 lap_transpose(n + AT_TRANSPOSE)
+            if last_graph(n + AT_TRANSPOSE + 1):
+                feat_sort(n + AT_TRANSPOSE + 1)
             if later_graph(n + AT_NODE_REGROUP):
                 node_regroup(n + AT_NODE_REGROUP)
-            if second_of_pair(n + AT_STORE):
+            if second_of_pair(n + AT_STORE) and n + AT_STORE < ALL_CHUNKS - 3:
                 output_store(n + AT_STORE)
 
             if valid(n + AT_LAP):
@@ -476,8 +523,12 @@ def tile_cheblayer_pb_t_kernel(tc, x, tx1, adj, W, b, out):
                 quantise(n + AT_QUANTISE, LAP, LAP + 1)
             elif valid(n + AT_TERM):
                 quantise(n + AT_QUANTISE, TX2, TX2 + 1)
+            if last_pair(n + AT_OUTPUT):
+                output_relu_direct(n + AT_OUTPUT)
             if later_graph(n + AT_NODE_QUANTISE) and second_of_pair(n + AT_NODE_QUANTISE):
                 node_quantise(n + AT_NODE_QUANTISE)
 
             if valid(n + AT_SECOND_ORDER):
                 second_order_products(n + AT_SECOND_ORDER)
+            if n + AT_RELU == ALL_CHUNKS - 3:
+                output_store(n + AT_RELU)

@@ -36,7 +36,7 @@ AT_QUANTISE = 4
 AT_TRANSPOSE = 5
 AT_LAP = 6
 AT_SPREAD = AT_LAP + 1
-AT_R = AT_LAP + 2
+AT_R = AT_LAP + 3
 AT_ROW_SUMS = AT_R + CHUNKS
 AT_NODE_QUANTISE = AT_SECOND_ORDER + CHUNKS
 AT_NODE_REGROUP = AT_NODE_QUANTISE + 1
@@ -67,7 +67,6 @@ def tile_cheblayer_pb_t_kernel(tc, x, tx1, adj, W, b, out):
         node_pool = pool("node", 5)
         short = pool("short", 3)
         lap_pool = pool("lap", LAP_BUFS)
-        sorted_pool = pool("sorted", 2)
         grouped_pool = pool("grouped", 5)
         codes_pool = pool("codes", 4)
         psum_t = stack.enter_context(tc.psum_pool(name="psum_t", bufs=4))
@@ -249,21 +248,11 @@ def tile_cheblayer_pb_t_kernel(tc, x, tx1, adj, W, b, out):
                 nc.tensor.transpose(out=bank[:, number, :], in_=words, identity=ident[:])
             return bank
 
-        sorted_rows = {}
-
-        def words_of(name, s):
-            return half_of(name, s)[:, s % HALF, :].bitcast(F32).rearrange("p (w u) -> p u w", u=2)
-
-        def feat_sort(s):
-            sorted_rows[s] = sorted_pool.tile([P, 2, 2, PASSES * P], F32, name="sorted")
-            for section, name in ((X, "x"), (TX1, "tx1")):
-                nc.scalar.copy(out=sorted_rows[s][:, section], in_=words_of(name, s))
-
         def feat_transpose(s):
             words = grouped_of(s)[:].bitcast(F32)
             for section, name in ((X, "x"), (TX1, "tx1")):
-                row = sorted_rows[s][:, section] if s in sorted_rows else words_of(name, s)
-                bank = transposed_words([row[:, u, a * P : (a + 1) * P] for a in range(PASSES) for u in range(2)])
+                row = half_of(name, s)[:, s % HALF, :].bitcast(F32).rearrange("p (a m u) -> p a u m", m=P, u=2)
+                bank = transposed_words([row[:, a, u] for a in range(PASSES) for u in range(2)])
                 nc.scalar.copy(out=words[:, section], in_=bank[:].rearrange("p (a u) i -> p a i u", u=2))
 
         def quantise(s, first, last):
@@ -437,7 +426,6 @@ def tile_cheblayer_pb_t_kernel(tc, x, tx1, adj, W, b, out):
 
         valid = lambda s: 0 <= s < ALL_CHUNKS
         last_pair = lambda s: ALL_CHUNKS - 2 <= s < ALL_CHUNKS
-        last_graph = lambda s: ALL_CHUNKS - CHUNKS <= s < ALL_CHUNKS
         later_graph = lambda s: CHUNKS <= s < ALL_CHUNKS
         first_of_half = lambda s: valid(s) and s % HALF == 0
         first_of_graph = lambda s: valid(s) and s % CHUNKS == 0
@@ -496,8 +484,6 @@ def tile_cheblayer_pb_t_kernel(tc, x, tx1, adj, W, b, out):
                 if n + AT_TRANSPOSE >= FEATS_EARLY:
                     feat_transpose(n + AT_TRANSPOSE)
                 lap_transpose(n + AT_TRANSPOSE)
-            if last_graph(n + AT_TRANSPOSE + 1):
-                feat_sort(n + AT_TRANSPOSE + 1)
             if later_graph(n + AT_NODE_REGROUP):
                 node_regroup(n + AT_NODE_REGROUP)
             if second_of_pair(n + AT_STORE) and n + AT_STORE < ALL_CHUNKS - 3:

@@ -67,6 +67,7 @@ def tile_cheblayer_pb_t_kernel(tc, x, tx1, adj, W, b, out):
         node_pool = pool("node", 5)
         short = pool("short", 3)
         lap_pool = pool("lap", LAP_BUFS)
+        sorted_pool = pool("sorted", 2)
         grouped_pool = pool("grouped", 5)
         codes_pool = pool("codes", 4)
         psum_t = stack.enter_context(tc.psum_pool(name="psum_t", bufs=4))
@@ -248,11 +249,21 @@ def tile_cheblayer_pb_t_kernel(tc, x, tx1, adj, W, b, out):
                 nc.tensor.transpose(out=bank[:, number, :], in_=words, identity=ident[:])
             return bank
 
+        sorted_rows = {}
+
+        def words_of(name, s):
+            return half_of(name, s)[:, s % HALF, :].bitcast(F32).rearrange("p (w u) -> p u w", u=2)
+
+        def feat_sort(s):
+            sorted_rows[s] = sorted_pool.tile([P, 2, 2, PASSES * P], F32, name="sorted")
+            for section, name in ((X, "x"), (TX1, "tx1")):
+                nc.scalar.copy(out=sorted_rows[s][:, section], in_=words_of(name, s))
+
         def feat_transpose(s):
             words = grouped_of(s)[:].bitcast(F32)
             for section, name in ((X, "x"), (TX1, "tx1")):
-                row = half_of(name, s)[:, s % HALF, :].bitcast(F32).rearrange("p (a m u) -> p a u m", m=P, u=2)
-                bank = transposed_words([row[:, a, u] for a in range(PASSES) for u in range(2)])
+                row = sorted_rows[s][:, section] if s in sorted_rows else words_of(name, s)
+                bank = transposed_words([row[:, u, a * P : (a + 1) * P] for a in range(PASSES) for u in range(2)])
                 nc.scalar.copy(out=words[:, section], in_=bank[:].rearrange("p (a u) i -> p a i u", u=2))
 
         def quantise(s, first, last):
@@ -425,6 +436,7 @@ def tile_cheblayer_pb_t_kernel(tc, x, tx1, adj, W, b, out):
             nc.sync.dma_start(out=rows[:, t : t + 2, :], in_=result[:])
 
         valid = lambda s: 0 <= s < ALL_CHUNKS
+        last_half = lambda s: ALL_CHUNKS - HALF <= s < ALL_CHUNKS
         last_pair = lambda s: ALL_CHUNKS - 2 <= s < ALL_CHUNKS
         later_graph = lambda s: CHUNKS <= s < ALL_CHUNKS
         first_of_half = lambda s: valid(s) and s % HALF == 0
@@ -473,6 +485,9 @@ def tile_cheblayer_pb_t_kernel(tc, x, tx1, adj, W, b, out):
 
             if second_of_pair(n + AT_RELU) and not last_pair(n + AT_RELU):
                 output_relu(n + AT_RELU)
+
+            if last_half(n + AT_TRANSPOSE + 1):
+                feat_sort(n + AT_TRANSPOSE + 1)
 
             if last_pair(n + AT_OUTPUT):
                 output_products_direct(n + AT_OUTPUT)

from contextlib import ExitStack

import concourse.mybir as mybir
from concourse.masks import make_identity

F32 = mybir.dt.float32
BF16 = mybir.dt.bfloat16
U32 = mybir.dt.uint32
U8 = mybir.dt.uint8
FP8X4 = mybir.dt.float8_e4m3fn_x4
ALU = mybir.AluOpType
ACT = mybir.ActivationFunctionType

P = 128
GRAPHS = 4
NODES = 1024
FEATS = 1024
OUT = 128
ORDERS = 3
EPS = 1e-6

BLOCK_BF16 = 16
PACK = 4
K_PASS = P * PACK
PASSES = NODES // K_PASS
CHUNKS = NODES // P
HALF = CHUNKS // PASSES
ALL_CHUNKS = GRAPHS * CHUNKS

AT_STORE = -1
AT_RELU = 0
AT_OUTPUT = 1
AT_TERM = 2
AT_SECOND_ORDER = 3
AT_QUANTISE = 4
AT_TRANSPOSE = 5
AT_LAP = 6
AT_SPREAD = AT_LAP + 1
AT_R = AT_LAP + 3
AT_ROW_SUMS = AT_R + CHUNKS
AT_NODE_QUANTISE = AT_SECOND_ORDER + CHUNKS
AT_NODE_REGROUP = AT_NODE_QUANTISE + 1
X, TX1, LAP, TX2 = 0, 1, 2, 3
TX2_LAG = AT_QUANTISE - AT_TERM
LOAD_AHEAD = 4
FEATS_EARLY = 1
ADJ_BUFS = 5
LAP_BUFS = AT_LAP - AT_TRANSPOSE + 1
TX1_BUFS = 4
X_BUFS = 2
assert AT_ROW_SUMS + LOAD_AHEAD <= AT_LAP + (ADJ_BUFS - 1) * HALF
assert AT_NODE_REGROUP + LOAD_AHEAD <= AT_TRANSPOSE + (TX1_BUFS - 1) * HALF
assert AT_TRANSPOSE + LOAD_AHEAD <= AT_TRANSPOSE + (X_BUFS - 1) * HALF

FLOPS = GRAPHS * (2 * NODES * NODES * FEATS + ORDERS * 2 * NODES * FEATS * OUT)


def tile_cheblayer_pb_t_kernel(tc, x, tx1, adj, W, b, out):
    nc = tc.nc
    with ExitStack() as stack:
        pool = lambda name, bufs: stack.enter_context(tc.tile_pool(name=name, bufs=bufs))
        const = pool("const", 1)
        adj_pool = pool("adj", ADJ_BUFS)
        tx1_pool = pool("tx1", TX1_BUFS)
        x_pool = pool("x", X_BUFS)
        graph_pool = pool("graph", 3)
        node_pool = pool("node", 5)
        short = pool("short", 3)
        lap_pool = pool("lap", LAP_BUFS)
        sorted_pool = pool("sorted", 2)
        grouped_pool = pool("grouped", 5)
        codes_pool = pool("codes", 4)
        psum_t = stack.enter_context(tc.psum_pool(name="psum_t", bufs=4))
        psum_m = stack.enter_context(tc.psum_pool(name="psum_m", bufs=2))
        psum_o = stack.enter_context(tc.psum_pool(name="psum_o", bufs=2))
        stack.enter_context(tc.manual_schedule())

        ident = const.tile([P, P], F32)
        make_identity(nc, ident[:])
        ident_bf = const.tile([P, P], BF16)
        make_identity(nc, ident_bf[:])
        eps = const.tile([P, 1], F32)
        nc.vector.memset(eps[:], EPS)
        warm = const.tile([P, 1], F32)
        nc.scalar.activation(out=warm[:], in_=eps[:], func=ACT.Abs_reciprocal_sqrt)

        halves = {}

        def load_half(name, src, tile_pool, q):
            g, h = q // CHUNKS, (q % CHUNKS) // HALF
            t = tile_pool.tile([P, HALF, FEATS], BF16, name=name)
            rows = src[g, h * K_PASS : (h + 1) * K_PASS, :].rearrange("(p t) f -> p t f", t=PACK)
            for c in range(0, HALF, 2):
                nc.sync.dma_start(out=t[:, c : c + 2, :], in_=rows[:, c : c + 2, :])
            halves[(name, g, h)] = t

        def half_of(name, s):
            return halves[(name, s // CHUNKS, (s % CHUNKS) // HALF)]

        w_raw = grouped_pool.tile([P, ORDERS * PASSES, PACK, OUT], BF16, name="grouped", align_bytes=64)
        w_grouped = grouped_pool.tile([P, ORDERS * PASSES, OUT, PACK], BF16, name="grouped", align_bytes=64)
        w_codes = const.tile([P, ORDERS, PASSES, OUT], U32, align_bytes=64)
        w_scales = const.tile([P, ORDERS, PASSES, OUT], U8, align_bytes=64)
        b_rows = const.tile([P, P], BF16)
        b_terms = const.tile([P, ORDERS], F32)
        bias_row = const.tile([P, OUT], F32)
        bias = const.tile([P, 1], F32)

        def load_weights():
            nc.sync.dma_start(
                out=w_raw[:].rearrange("p a t o -> p a (t o)"),
                in_=W.rearrange("k (a p t) o -> p (k a) (t o)", p=P, t=PACK),
            )
            nc.vector.memset(b_rows[:], 0.0)
            nc.sync.dma_start(out=b_rows[0:ORDERS, :], in_=b)

        def quantise_weights():
            nc.vector.tensor_copy(out=w_grouped[:], in_=w_raw[:].rearrange("p a t o -> p a o t"))
            for k in range(ORDERS):
                nc.vector.quantize_mx(
                    out=w_codes[:, k].rearrange("p a o -> p (a o)").bitcast(FP8X4),
                    scales=w_scales[:, k].rearrange("p a o -> p (a o)"),
                    in_=w_grouped[:, k * PASSES : (k + 1) * PASSES].rearrange("p a o t -> p (a o t)"),
                )
            b_cols = psum_t.tile([P, P], BF16, name="bank")
            nc.tensor.transpose(out=b_cols[:], in_=b_rows[:], identity=ident_bf[:])
            nc.scalar.activation(out=b_terms[:], in_=b_cols[:, 0:ORDERS], func=ACT.Copy, accum_out=bias[:, 0:1])
            b_spread = psum_t.tile([P, OUT], F32, name="bank")
            nc.tensor.transpose(out=b_spread[:], in_=bias[:, 0:1].to_broadcast([P, OUT]), identity=ident[:])
            nc.scalar.copy(out=bias_row[:], in_=b_spread[:])

        vectors = {g: {} for g in range(GRAPHS)}
        node_codes = {}
        node_grouped = {}

        def node_regroup(q):
            j, w = q % HALF, q % 2
            if w == 0:
                node_grouped[q // 2] = short.tile([P, PACK, P, PACK], BF16, name="node_grouped", align_bytes=64)
            words = slice(w * P // 2, (w + 1) * P // 2)
            grouped = node_grouped[q // 2][:, :, words, :].rearrange("p v m t -> p m t v")
            rows = half_of("tx1", q)[:, :, j * 2 * P : (j + 1) * 2 * P].rearrange("p t (m v) -> p m t v", v=PACK)
            if q < CHUNKS:
                nc.vector.tensor_copy(out=grouped, in_=rows)
            else:
                nc.scalar.copy(out=grouped, in_=rows)

        def node_quantise(q):
            key = (q // CHUNKS, (q % CHUNKS) // HALF)
            if q % HALF == 1:
                node_codes[key] = (
                    node_pool.tile([P, FEATS], U32, name="node_c", align_bytes=64),
                    node_pool.tile([P, FEATS], U8, name="node_s", align_bytes=64),
                )
            codes, scales = node_codes[key]
            windows = slice((q % HALF - 1) * 2 * P, (q % HALF + 1) * 2 * P)
            nc.vector.quantize_mx(
                out=codes[:, windows].bitcast(FP8X4),
                scales=scales[:, windows],
                in_=node_grouped[q // 2][:].rearrange("p v m t -> p (v m t)"),
            )

        def row_sums(q):
            g, k = q // CHUNKS, q % CHUNKS
            if k == 0:
                vectors[g]["d"] = graph_pool.tile([P, CHUNKS], F32, name="d")
            d = vectors[g]["d"][:, k : k + 1]
            row = half_of("adj", q)[:, q % HALF, :]
            if k % 2 == 0:
                junk = short.tile([P, NODES], BF16, name="junk_row")
                nc.scalar.activation(out=junk[:], in_=row, func=ACT.Copy, accum_out=d)
            else:
                folded = psum_t.tile([P, P], F32, name="bank")
                for blk in range(CHUNKS):
                    nc.tensor.matmul(
                        out=folded[:],
                        lhsT=ident_bf[:],
                        rhs=row[:, blk * P : (blk + 1) * P],
                        start=(blk == 0),
                        stop=(blk == CHUNKS - 1),
                    )
                junk = short.tile([P, P], F32, name="junk")
                nc.scalar.activation(out=junk[:], in_=folded[:], func=ACT.Copy, accum_out=d)

        def vectors_r(g):
            vectors[g]["r"] = graph_pool.tile([P, CHUNKS], F32, name="r")
            nc.scalar.activation(
                out=vectors[g]["r"][:], in_=vectors[g]["d"][:], func=ACT.Abs_reciprocal_sqrt, bias=eps[:, 0:1]
            )

        def load_diagonal(g):
            vectors[g]["a_diag"] = graph_pool.tile([P, 2, BLOCK_BF16], BF16, name="a_diag")
            diagonal = adj[g].rearrange("i j -> (i j)")[0 : NODES * NODES : NODES + 1]
            with nc.allow_non_contiguous_dma(reason="1,024 single elements, one from each row of adj"):
                for h in range(PASSES):
                    nc.sync.dma_start(
                        out=vectors[g]["a_diag"][:, h, 0:HALF],
                        in_=diagonal.rearrange("(h p t) -> h p t", p=P, t=HALF)[h],
                    )

        def vectors_diagonal(g):
            v = vectors[g]
            small = lambda name, dtype: graph_pool.tile([P, CHUNKS], dtype, name=name)
            half_product, product, stored, one_less = (
                small("half_product", F32), small("product", F32), small("stored", BF16), small("one_less", F32)
            )
            v["eye_fix"] = small("eye_fix", F32)
            by_half = lambda ap: ap.rearrange("p (h t) -> p h t", t=HALF)
            nc.gpsimd.tensor_tensor(
                out=by_half(half_product[:]),
                in0=v["a_diag"][:, :, 0:HALF],
                in1=by_half(v["r"][:]),
                op=ALU.mult,
            )
            nc.gpsimd.tensor_tensor(out=product[:], in0=half_product[:], in1=v["r"][:], op=ALU.mult)
            nc.gpsimd.tensor_copy(out=stored[:], in_=product[:])
            nc.gpsimd.tensor_scalar(
                out=one_less[:], in0=product[:], scalar1=-1.0, scalar2=1.0, op0=ALU.mult, op1=ALU.add
            )
            nc.gpsimd.tensor_tensor(out=v["eye_fix"][:], in0=one_less[:], in1=stored[:], op=ALU.add)

        def vectors_spread(g):
            v = vectors[g]
            v["neg_r_cols"] = graph_pool.tile([P, 2, PASSES, P, 2], F32, name="neg_r_cols")
            for h in range(PASSES):
                spread = psum_t.tile([P, HALF, P], F32, name="bank")
                for j in range(HALF):
                    k = h * HALF + j
                    nc.tensor.transpose(
                        out=spread[:, j, :], in_=v["r"][:, k : k + 1].to_broadcast([P, P]), identity=ident[:]
                    )
                nc.scalar.activation(
                    out=v["neg_r_cols"][:, :, h],
                    in_=spread[:].rearrange("p (u e) m -> p u m e", e=2),
                    func=ACT.Copy,
                    scale=-1.0,
                )

        chunks = {s: {} for s in range(ALL_CHUNKS + TX2_LAG)}

        def grouped_of(s):
            if "grouped" not in chunks[s]:
                chunks[s]["grouped"] = grouped_pool.tile([P, 4, PASSES, P, PACK], BF16, name="grouped", align_bytes=64)
            return chunks[s]["grouped"]

        def transposed_words(planes):
            bank = psum_t.tile([P, PACK, P], F32, name="bank")
            for number, words in enumerate(planes):
                nc.tensor.transpose(out=bank[:, number, :], in_=words, identity=ident[:])
            return bank

        sorted_rows = {}

        def words_of(name, s):
            return half_of(name, s)[:, s % HALF, :].bitcast(F32).rearrange("p (w u) -> p u w", u=2)

        def feat_sort(s):
            sorted_rows[s] = sorted_pool.tile([P, 2, 2, PASSES * P], F32, name="sorted")
            for section, name in ((X, "x"), (TX1, "tx1")):
                nc.scalar.copy(out=sorted_rows[s][:, section], in_=words_of(name, s))

        def feat_transpose(s):
            words = grouped_of(s)[:].bitcast(F32)
            for section, name in ((X, "x"), (TX1, "tx1")):
                row = sorted_rows[s][:, section] if s in sorted_rows else words_of(name, s)
                bank = transposed_words([row[:, u, a * P : (a + 1) * P] for a in range(PASSES) for u in range(2)])
                nc.scalar.copy(out=words[:, section], in_=bank[:].rearrange("p (a u) i -> p a i u", u=2))

        def quantise(s, first, last):
            t = chunks[s]
            if "codes" not in t:
                t["codes"] = codes_pool.tile([P, 4, PASSES, P], U32, name="codes", align_bytes=64)
                t["scales"] = codes_pool.tile([P, 4, PASSES, P], U8, name="scales", align_bytes=64)
            nc.vector.quantize_mx(
                out=t["codes"][:, first:last].rearrange("p m a i -> p (m a i)").bitcast(FP8X4),
                scales=t["scales"][:, first:last].rearrange("p m a i -> p (m a i)"),
                in_=t["grouped"][:, first:last].rearrange("p m a i t -> p (m a i t)"),
            )

        lap_tiles = {}

        def diagonal_plane(s):
            return s % HALF // 2

        def lap_rows(s, u):
            k = s % CHUNKS
            v = vectors[s // CHUNKS]
            if s not in lap_tiles:
                lap_tiles[s] = lap_pool.tile([P, 2, PASSES * P, 2], BF16, name="lap")
            columns = half_of("adj", s)[:, s % HALF, :].rearrange("p (m u e) -> p u m e", u=2, e=2)
            nc.vector.scalar_tensor_tensor(
                out=lap_tiles[s][:, u],
                in0=columns[:, u],
                scalar=v["r"][:, k : k + 1],
                in1=v["neg_r_cols"][:, u].rearrange("p a m e -> p (a m) e"),
                op0=ALU.mult,
                op1=ALU.mult,
            )

        eye_rows = {}

        def lap_eye_row(s):
            eye_rows[s] = short.tile([P, P], F32, name="eye_row")
            k = s % CHUNKS
            nc.gpsimd.tensor_scalar(
                out=eye_rows[s][:],
                in0=ident[:],
                scalar1=vectors[s // CHUNKS]["eye_fix"][:, k : k + 1],
                scalar2=0.0,
                op0=ALU.mult,
                op1=ALU.add,
            )

        def lap_add_eye_vector(s):
            k = s % CHUNKS
            h = k // HALF
            diag_cols = lap_tiles[s][:, diagonal_plane(s), h * P : (h + 1) * P, k % 2]
            nc.vector.scalar_tensor_tensor(
                out=diag_cols,
                in0=ident[:],
                scalar=vectors[s // CHUNKS]["eye_fix"][:, k : k + 1],
                in1=diag_cols,
                op0=ALU.mult,
                op1=ALU.add,
            )

        def lap_add_eye(s):
            k = s % CHUNKS
            h = k // HALF
            diag_cols = lap_tiles[s][:, diagonal_plane(s), h * P : (h + 1) * P, k % 2]
            nc.gpsimd.tensor_tensor(out=diag_cols, in0=eye_rows.pop(s)[:], in1=diag_cols, op=ALU.add)

        def lap_transpose(s):
            row = lap_tiles.pop(s)[:].bitcast(F32).rearrange("p u (a m) o -> p u a (m o)", m=P)
            bank = transposed_words([row[:, u, a] for a in range(PASSES) for u in range(2)])
            words = grouped_of(s)[:].bitcast(F32)
            nc.scalar.copy(out=words[:, LAP], in_=bank[:].rearrange("p (a u) i -> p a i u", u=2))

        def second_order_products(s):
            t = chunks[s]
            t["acc"] = []
            for a in range(PASSES):
                acc = psum_m.tile([P, PACK, P], F32, name="acc")
                t["acc"].append(acc)
                for v in range(PACK):
                    cols = slice((a * PACK + v) * P, (a * PACK + v + 1) * P)
                    for h in range(PASSES):
                        codes, scales = node_codes[(s // CHUNKS, h)]
                        nc.tensor.matmul_mx(
                            out=acc[:, v, :],
                            lhsT=codes[:, cols].bitcast(FP8X4),
                            lhsT_scale=scales[:, cols],
                            rhs=t["codes"][:, LAP, h, :].bitcast(FP8X4),
                            rhs_scale=t["scales"][:, LAP, h, :],
                            start=(h == 0),
                            stop=(h == PASSES - 1),
                        )

        def second_order_term(s, a):
            nc.vector.scalar_tensor_tensor(
                out=grouped_of(s + TX2_LAG)[:, TX2, a],
                in0=chunks[s]["acc"][a][:].rearrange("p v i -> p i v"),
                scalar=2.0,
                in1=grouped_of(s)[:, X, a],
                op0=ALU.mult,
                op1=ALU.subtract,
            )

        pair_acc = {}

        def output_products_direct(s):
            t, later = chunks[s], chunks[s + TX2_LAG]
            if s % 2 == 0:
                pair_acc[s // 2] = psum_o.tile([P, 2, P], F32, name="out_acc")
            acc = pair_acc[s // 2][:, s % 2, :]
            operands = [
                (t["codes"][:, X], t["scales"][:, X]),
                (t["codes"][:, TX1], t["scales"][:, TX1]),
                (later["codes"][:, TX2], later["scales"][:, TX2]),
            ]
            for k, (codes, scales) in enumerate(operands):
                for a in range(PASSES):
                    nc.tensor.matmul_mx(
                        out=acc,
                        lhsT=codes[:, a, :].bitcast(FP8X4),
                        lhsT_scale=scales[:, a, :],
                        rhs=w_codes[:, k, a, :].bitcast(FP8X4),
                        rhs_scale=w_scales[:, k, a, :],
                        start=(k == 0 and a == 0),
                        stop=(k == ORDERS - 1 and a == PASSES - 1),
                    )

        def output_relu_direct(s):
            total = short.tile([P, OUT], F32, name="total")
            nc.vector.tensor_tensor(out=total[:], in0=pair_acc[s // 2][:, s % 2, :], in1=bias_row[:], op=ALU.add)
            result = short.tile([P, OUT], F32, name="result_direct")
            nc.vector.tensor_scalar_max(out=result[:], in0=total[:], scalar1=0.0)
            g, h = s // CHUNKS, (s % CHUNKS) // HALF
            rows = out[g, h * K_PASS : (h + 1) * K_PASS, :].rearrange("(p t) o -> p t o", t=HALF)
            nc.sync.dma_start(out=rows[:, s % HALF, :], in_=result[:])

        def output_products(s):
            t = chunks[s]
            if s % 2 == 0:
                pair_acc[s // 2] = psum_o.tile([P, 2, P], F32, name="out_acc")
            later = chunks[s + TX2_LAG]
            operands = [
                (t["codes"][:, X], t["scales"][:, X]),
                (t["codes"][:, TX1], t["scales"][:, TX1]),
                (later["codes"][:, TX2], later["scales"][:, TX2]),
            ]
            for k, (codes, scales) in enumerate(operands):
                for a in range(PASSES):
                    nc.tensor.matmul_mx(
                        out=pair_acc[s // 2][:, s % 2, :],
                        lhsT=w_codes[:, k, a, :].bitcast(FP8X4),
                        lhsT_scale=w_scales[:, k, a, :],
                        rhs=codes[:, a, :].bitcast(FP8X4),
                        rhs_scale=scales[:, a, :],
                        start=(k == 0 and a == 0),
                        stop=(k == ORDERS - 1 and a == PASSES - 1),
                    )

        def output_relu(s):
            chunks[s]["relu"] = short.tile([P, 2, P], F32, name="relu")
            nc.scalar.activation(out=chunks[s]["relu"][:], in_=pair_acc[s // 2][:], func=ACT.Relu, bias=bias[:, 0:1])

        def output_store(s):
            g, h, t = s // CHUNKS, (s % CHUNKS) // HALF, s % HALF - 1
            bank = psum_t.tile([P, 2, OUT], F32, name="bank")
            for e in range(2):
                nc.tensor.transpose(out=bank[:, e, :], in_=chunks[s]["relu"][:, e, :], identity=ident[:])
            result = short.tile([P, 2, OUT], F32, name="result")
            nc.scalar.copy(out=result[:], in_=bank[:])
            rows = out[g, h * K_PASS : (h + 1) * K_PASS, :].rearrange("(p t) o -> p t o", t=HALF)
            nc.sync.dma_start(out=rows[:, t : t + 2, :], in_=result[:])

        valid = lambda s: 0 <= s < ALL_CHUNKS
        last_half = lambda s: ALL_CHUNKS - HALF <= s < ALL_CHUNKS
        last_pair = lambda s: ALL_CHUNKS - 2 <= s < ALL_CHUNKS
        later_graph = lambda s: CHUNKS <= s < ALL_CHUNKS
        first_of_half = lambda s: valid(s) and s % HALF == 0
        first_of_graph = lambda s: valid(s) and s % CHUNKS == 0
        second_of_pair = lambda s: valid(s) and s % 2 == 1

        first_step = -(AT_ROW_SUMS + LOAD_AHEAD - CHUNKS)
        load_half("tx1", tx1, tx1_pool, 0)
        load_half("adj", adj, adj_pool, 0)
        load_half("tx1", tx1, tx1_pool, HALF)
        load_half("adj", adj, adj_pool, HALF)
        load_diagonal(0)
        load_weights()
        load_half("x", x, x_pool, 0)
        for q in range(HALF):
            node_regroup(q)
            row_sums(q)
            if q % 2 == 1:
                node_quantise(q)
        for q in range(HALF, CHUNKS):
            node_regroup(q)
            row_sums(q)
            if q % 2 == 1:
                node_quantise(q)
        vectors_r(0)
        vectors_spread(0)
        vectors_diagonal(0)
        for s in range(FEATS_EARLY):
            feat_transpose(s)
        quantise_weights()
        for n in range(first_step, ALL_CHUNKS - AT_STORE):
            if first_of_half(n + AT_TRANSPOSE + LOAD_AHEAD) and n + AT_TRANSPOSE + LOAD_AHEAD > 0:
                load_half("x", x, x_pool, n + AT_TRANSPOSE + LOAD_AHEAD)
            if later_graph(n + AT_NODE_REGROUP + LOAD_AHEAD) and first_of_half(n + AT_NODE_REGROUP + LOAD_AHEAD):
                load_half("tx1", tx1, tx1_pool, n + AT_NODE_REGROUP + LOAD_AHEAD)
            if later_graph(n + AT_ROW_SUMS + LOAD_AHEAD) and first_of_half(n + AT_ROW_SUMS + LOAD_AHEAD):
                load_half("adj", adj, adj_pool, n + AT_ROW_SUMS + LOAD_AHEAD)
            if later_graph(n + AT_ROW_SUMS) and first_of_graph(n + AT_ROW_SUMS):
                load_diagonal((n + AT_ROW_SUMS) // CHUNKS)

            if later_graph(n + AT_R) and first_of_graph(n + AT_R):
                vectors_r((n + AT_R) // CHUNKS)
            if later_graph(n + AT_SPREAD) and first_of_graph(n + AT_SPREAD):
                vectors_spread((n + AT_SPREAD) // CHUNKS)
                vectors_diagonal((n + AT_SPREAD) // CHUNKS)

            if second_of_pair(n + AT_RELU) and not last_pair(n + AT_RELU):
                output_relu(n + AT_RELU)

            if last_half(n + AT_TRANSPOSE + 1):
                feat_sort(n + AT_TRANSPOSE + 1)

            if last_pair(n + AT_OUTPUT):
                output_products_direct(n + AT_OUTPUT)
            elif valid(n + AT_OUTPUT):
                output_products(n + AT_OUTPUT)
            if later_graph(n + AT_ROW_SUMS):
                row_sums(n + AT_ROW_SUMS)
            if valid(n + AT_TRANSPOSE):
                if n + AT_TRANSPOSE >= FEATS_EARLY:
                    feat_transpose(n + AT_TRANSPOSE)
                lap_transpose(n + AT_TRANSPOSE)
            if later_graph(n + AT_NODE_REGROUP):
                node_regroup(n + AT_NODE_REGROUP)
            if second_of_pair(n + AT_STORE) and n + AT_STORE < ALL_CHUNKS - 3:
                output_store(n + AT_STORE)

            if valid(n + AT_LAP):
                lap_rows(n + AT_LAP, diagonal_plane(n + AT_LAP))
                if valid(n + AT_TERM):
                    lap_add_eye(n + AT_LAP)
            if valid(n + AT_LAP + 1) and valid(n + AT_TERM + 1):
                lap_eye_row(n + AT_LAP + 1)
            if valid(n + AT_TERM):
                second_order_term(n + AT_TERM, 0)
                second_order_term(n + AT_TERM, 1)
            if valid(n + AT_LAP):
                lap_rows(n + AT_LAP, 1 - diagonal_plane(n + AT_LAP))
                if not valid(n + AT_TERM):
                    lap_add_eye_vector(n + AT_LAP)
            if valid(n + AT_QUANTISE) and valid(n + AT_TERM):
                quantise(n + AT_QUANTISE, X, TX2 + 1)
            elif valid(n + AT_QUANTISE):
                quantise(n + AT_QUANTISE, X, TX1 + 1)
                quantise(n + AT_QUANTISE, LAP, LAP + 1)
            elif valid(n + AT_TERM):
                quantise(n + AT_QUANTISE, TX2, TX2 + 1)
            if last_pair(n + AT_OUTPUT):
                output_relu_direct(n + AT_OUTPUT)
            if later_graph(n + AT_NODE_QUANTISE) and second_of_pair(n + AT_NODE_QUANTISE):
                node_quantise(n + AT_NODE_QUANTISE)

            if valid(n + AT_SECOND_ORDER):
                second_order_products(n + AT_SECOND_ORDER)
            if n + AT_RELU == ALL_CHUNKS - 3:
                output_store(n + AT_RELU)
